import numpy as np
import ml_dtypes


def mxq(x, axis, fmt="e4m3"):
    dtype, down = {"e4m3": (ml_dtypes.float8_e4m3fn, 7), "e5m2": (ml_dtypes.float8_e5m2, 14)}[fmt]
    v = np.moveaxis(np.asarray(x, np.float32).astype(ml_dtypes.bfloat16).astype(np.float64), axis, -1)
    blocks = v.reshape(v.shape[:-1] + (-1, 32))
    amax = np.abs(blocks).max(-1, keepdims=True)
    byte = np.maximum(np.where(amax > 0, np.frexp(amax)[1] - 1 + 127, 0) - down, 1)
    scale = np.exp2(byte - 127.0)
    codes = (blocks / scale).astype(np.float32).astype(dtype).astype(np.float64)
    return np.moveaxis((codes * scale).reshape(v.shape), -1, axis)


WIDE = False


def mx_kscale(k):
    if not WIDE:
        return np.ones(k)
    levels = np.array([10, -10, 5, -5, 0])
    a = np.random.permutation(np.resize(levels, k // 512 * 4)).reshape(k // 512, 4)
    idx = np.arange(k)
    return np.exp2(a[idx // 512, idx % 128 // 32])


BF16 = ml_dtypes.bfloat16


def bf(x):
    return np.asarray(x, np.float32).astype(BF16)


def f64(x):
    return np.asarray(x).astype(np.float64)


B, T, D, F = 32, 128, 512, 256
K2, K3, K4 = 2, 3, 4
EPS = 1e-12


def conv_branch(xq, w, b):
    kw = w.shape[1]
    n = xq.shape[1] - kw + 1
    wq = mxq(f64(w), 2, "e4m3")
    out = sum((xq[:, k:k + n, :] @ wq[:, k, :].T) for k in range(kw))
    return np.maximum(out + f64(b), 0.0)


def l2norm(x, axis):
    n = np.sqrt(np.sum(x * x, axis=axis, keepdims=True))
    return x / np.maximum(n, EPS)


def setup_inputs():
    s = mx_kscale(D)
    return {"words_emb": bf(np.random.standard_normal((B, T, D)) * s),
            "W2": bf(np.random.standard_normal((F, K2, D)) / np.sqrt(K2 * D) / s), "b2": bf(np.random.standard_normal(F) * 0.3),
            "W3": bf(np.random.standard_normal((F, K3, D)) / np.sqrt(K3 * D) / s), "b3": bf(np.random.standard_normal(F) * 0.3),
            "W4": bf(np.random.standard_normal((F, K4, D)) / np.sqrt(K4 * D) / s), "b4": bf(np.random.standard_normal(F) * 0.3)}


def reference(words_emb, W2, b2, W3, b3, W4, b4):
    xq = mxq(f64(words_emb), 2, "e4m3")
    a = conv_branch(xq, W2, b2)
    b_ = conv_branch(xq, W3, b3)
    c = conv_branch(xq, W4, b4)
    seq = T - K4 + 1
    main = np.maximum(np.maximum(a[:, :seq], b_[:, :seq]), c[:, :seq])
    pen = np.maximum(a[:, seq], b_[:, seq])[:, None]
    last = a[:, seq + 1][:, None]
    code = np.concatenate([main, pen, last], axis=1)
    code = l2norm(code, 2)
    return code.transpose(0, 2, 1)

@@ -1,0 +1,242 @@
+from contextlib import ExitStack
+
+import concourse.mybir as mybir
+from concourse.masks import make_identity
+
+F32 = mybir.dt.float32
+BF16 = mybir.dt.bfloat16
+U32 = mybir.dt.uint32
+U8 = mybir.dt.uint8
+FP8X4 = mybir.dt.float8_e4m3fn_x4
+ACT = mybir.ActivationFunctionType
+ALU = mybir.AluOpType
+
+P = 128
+B, T, D, F = 32, 128, 512, 256
+WIDTHS = (4, 3, 2)
+NB = 4
+G = B // NB
+L = 8
+PH = T // L
+BLK = NB * PH
+HALO = 4
+NCOL = (L + HALO) * BLK
+UNIT0 = {4: 0, 3: 4, 2: 7}
+BIAS_COL = {4: 0, 3: 2, 2: 4}
+FLOPS = 2 * B * D * F * (2 * 127 + 3 * 126 + 4 * 125)
+
+
+def tile_textheading_pa_t_kernel(tc, words_emb, W2, b2, W3, b3, W4, b4, out):
+    nc = tc.nc
+    w_dram = {2: W2, 3: W3, 4: W4}
+    b_dram = {2: b2, 3: b3, 4: b4}
+    with ExitStack() as ctx:
+        const = ctx.enter_context(tc.tile_pool(name="const", bufs=1))
+        raw = ctx.enter_context(tc.tile_pool(name="raw", bufs=1))
+        xq = ctx.enter_context(tc.tile_pool(name="xq", bufs=3))
+        xg = ctx.enter_context(tc.tile_pool(name="xg", bufs=2))
+        code_pool = ctx.enter_context(tc.tile_pool(name="code", bufs=4))
+        work = ctx.enter_context(tc.tile_pool(name="work", bufs=2))
+        split = ctx.enter_context(tc.tile_pool(name="split", bufs=4))
+        outp = ctx.enter_context(tc.tile_pool(name="outp", bufs=3))
+        mxp = ctx.enter_context(tc.psum_pool(name="mxp", bufs=2))
+        aux = ctx.enter_context(tc.psum_pool(name="aux", bufs=2))
+
+        one_col = const.tile([P, 1], F32, name="one_col")
+        nc.vector.memset(one_col[:], 1.0)
+        dummy = const.tile([P, 1], F32, name="dummy")
+        nc.scalar.activation(out=dummy[:], in_=one_col[:], func=ACT.Abs_reciprocal_sqrt)
+        ident = const.tile([P, P], F32, name="ident")
+        make_identity(nc, ident[:])
+        ident_bf = const.tile([P, P], BF16, name="ident_bf")
+        nc.vector.tensor_copy(out=ident_bf[:], in_=ident[:])
+        ones_bf = const.tile([P, P], BF16, name="ones_bf")
+        nc.vector.memset(ones_bf[:], 1.0)
+        bias_rows = const.tile([P, P], BF16, name="bias_rows")
+        nc.vector.memset(bias_rows[:], 0.0)
+        halos = []
+        for i in range(2):
+            halo = const.tile([P, HALO * BLK * 4], BF16, name="halo%d" % i, align_bytes=64)
+            nc.vector.memset(halo[:], 0.0)
+            halos.append(halo)
+
+        for K in WIDTHS:
+            c = BIAS_COL[K]
+            nc.scalar.dma_start(out=bias_rows[c : c + 2, :], in_=b_dram[K].rearrange("(h f) -> h f", h=2))
+        x_raw = []
+        w_raw = {}
+
+        def load_x(g):
+            t = raw.tile([P, NB, D], BF16, name="x_raw%d" % g)
+            nc.sync.dma_start(out=t[:], in_=words_emb[g * NB : (g + 1) * NB].rearrange("n p d -> p n d"))
+            x_raw.append(t)
+
+        load_x(0)
+        for h in range(2):
+            for K in WIDTHS:
+                t = raw.tile([P, K * D], BF16, name="w_raw%d_%d" % (K, h))
+                nc.sync.dma_start(out=t[:], in_=w_dram[K][h * P : (h + 1) * P].rearrange("f k d -> f (k d)"))
+                w_raw[(K, h)] = t
+        for g in range(1, G):
+            load_x(g)
+
+        w_codes = const.tile([P, 18 * P], U32, name="w_codes", align_bytes=64)
+        w_scales = const.tile([P, 18 * P], U8, name="w_scales", align_bytes=64)
+        bias_sb = const.tile([P, 6], F32, name="bias_sb")
+
+        flip = [0]
+
+        def copy_out(out_ap, in_ap):
+            if flip[0] % 2 == 0:
+                nc.scalar.copy(out=out_ap, in_=in_ap)
+            else:
+                nc.vector.tensor_copy(out=out_ap, in_=in_ap)
+            flip[0] += 1
+
+        bank_tags = ["c4", "c3", "c2"]
+        bank_no = [0]
+
+        def prep_w(h):
+            for K in WIDTHS:
+                words = w_raw[(K, h)][:].bitcast(F32)
+                grp = raw.tile([P, K * D], BF16, name="w_grp%d_%d" % (K, h), align_bytes=64)
+                grp_w = grp[:].bitcast(F32).rearrange("q (c f u) -> q c f u", c=K, f=P, u=2)
+                for k0 in range(0, K, 2):
+                    cnt = min(2, K - k0)
+                    ps = mxp.tile([P, 4, P], F32, name="ps_w", tag=bank_tags[bank_no[0] % 3])
+                    bank_no[0] += 1
+                    for i in range(cnt):
+                        for u in range(2):
+                            col = (k0 + i) * 256 + u * P
+                            nc.tensor.transpose(ps[:, 2 * i + u, :], words[:, col : col + P], ident[:])
+                    copy_out(
+                        grp_w[:, k0 : k0 + cnt],
+                        ps[:, 0 : 2 * cnt, :].rearrange("q (c u) f -> q c f u", u=2),
+                    )
+                unit = h * 9 + UNIT0[K]
+                for k0, cnt in {4: ((0, 4),), 3: ((0, 2), (2, 1)), 2: ((0, 2),)}[K]:
+                    cols = slice((unit + k0) * P, (unit + k0 + cnt) * P)
+                    nc.vector.quantize_mx(
+                        out=w_codes[:, cols].bitcast(FP8X4),
+                        scales=w_scales[:, cols],
+                        in_=grp[:, k0 * D : (k0 + cnt) * D],
+                    )
+
+        x_codes = {}
+        x_scales = {}
+
+        def prep_x(g):
+            words = x_raw[g][:].bitcast(F32)
+            grp = xg.tile([P, L * BLK * 4], BF16, name="x_grp", align_bytes=64)
+            grp_w = grp[:].bitcast(F32)
+            grp_v = grp_w.rearrange("q (pl n ph u) -> q pl n ph u", pl=L, n=NB, ph=PH, u=2)
+            for n0 in range(0, NB, 2):
+                ps = aux.tile([P, 4, P], F32, name="ps_x", tag="aux")
+                for i in range(2):
+                    for u in range(2):
+                        nc.tensor.transpose(ps[:, 2 * i + u, :], words[:, n0 + i, u * P : (u + 1) * P], ident[:])
+                for i in range(2):
+                    nc.scalar.copy(
+                        out=grp_v[:, :, n0 + i, :, :],
+                        in_=ps[:, 2 * i : 2 * i + 2, :].rearrange("q u (ph pl) -> q pl ph u", pl=L),
+                    )
+            halo = halos[g % 2]
+            rows = 3 * NB
+            nc.vector.tensor_copy(
+                out=halo[:].bitcast(F32).rearrange("q (r w) -> q r w", w=2 * PH)[:, 0:rows, 0 : 2 * PH - 2],
+                in_=grp_w.rearrange("q (r w) -> q r w", w=2 * PH)[:, 0:rows, 2 : 2 * PH],
+            )
+            xc = xq.tile([P, NCOL], U32, name="x_codes", align_bytes=64)
+            xs = xq.tile([P, NCOL], U8, name="x_scales", align_bytes=64)
+            nc.vector.quantize_mx(out=xc[:, 0 : L * BLK].bitcast(FP8X4), scales=xs[:, 0 : L * BLK], in_=grp[:])
+            nc.vector.quantize_mx(out=xc[:, L * BLK : NCOL].bitcast(FP8X4), scales=xs[:, L * BLK : NCOL], in_=halo[:])
+            x_codes[g] = xc
+            x_scales[g] = xs
+
+        codes = {}
+
+        def mx(g, h):
+            xc = x_codes[g]
+            xs = x_scales[g]
+            code = code_pool.tile([P, NB * T], F32, name="code%d" % h)
+            code_v = code[:].rearrange("f (m pl) -> f m pl", pl=L)
+            code_p = code[:].rearrange("f (n p) -> f n p", p=T)
+            for K in WIDTHS:
+                acc = mxp.tile([P, 512], F32, name="acc", tag="c%d" % K)
+                for k in range(K):
+                    unit = h * 9 + UNIT0[K] + k
+                    nc.tensor.matmul_mx(
+                        out=acc[:],
+                        lhsT=w_codes[:, unit * P : (unit + 1) * P].bitcast(FP8X4),
+                        lhsT_scale=w_scales[:, unit * P : (unit + 1) * P],
+                        rhs=xc[:, k * BLK : k * BLK + 512].bitcast(FP8X4),
+                        rhs_scale=xs[:, k * BLK : k * BLK + 512],
+                        start=(k == 0),
+                        stop=(k == K - 1),
+                    )
+                acc_v = acc[:].rearrange("f (pl m) -> f m pl", pl=L)
+                bias = bias_sb[:, BIAS_COL[K] + h : BIAS_COL[K] + h + 1]
+                if K == 4:
+                    nc.scalar.activation(out=code_v, in_=acc_v, func=ACT.Relu, bias=bias)
+                else:
+                    nc.vector.memset(code_p[:, :, T - K : T], 0.0)
+                    nc.vector.scalar_tensor_tensor(
+                        out=code_v, in0=acc_v, scalar=bias, in1=code_v, op0=ALU.add, op1=ALU.max
+                    )
+            codes[(g, h)] = code
+
+        parts = {}
+
+        def norm_a(g):
+            sq = []
+            for h in range(2):
+                s = work.tile([P, NB * T], F32, name="sq%d" % h)
+                nc.scalar.activation(out=s[:], in_=codes[(g, h)][:], func=ACT.Square)
+                sq.append(s)
+            tot = work.tile([P, NB * T], F32, name="tot")
+            nc.gpsimd.tensor_tensor(out=tot[:], in0=sq[0][:], in1=sq[1][:], op=ALU.add)
+            hi = split.tile([P, NB * T], BF16, name="hi")
+            nc.scalar.copy(out=hi[:], in_=tot[:])
+            lo = split.tile([P, NB * T], BF16, name="lo")
+            nc.gpsimd.tensor_tensor(out=lo[:], in0=tot[:], in1=hi[:], op=ALU.subtract)
+            parts[g] = (hi, lo)
+
+        def norm_b(g):
+            hi, lo = parts[g]
+            ss = aux.tile([P, NB * T], F32, name="ss", tag="aux")
+            nc.tensor.matmul(out=ss[:], lhsT=ones_bf[:], rhs=hi[:], start=True, stop=False)
+            nc.tensor.matmul(out=ss[:], lhsT=ones_bf[:], rhs=lo[:], start=False, stop=True)
+            rinv = work.tile([P, NB * T], F32, name="rinv")
+            nc.scalar.activation(out=rinv[:], in_=ss[:], func=ACT.Abs_reciprocal_sqrt)
+            for h in range(2):
+                o = outp.tile([P, NB, T], F32, name="o%d" % h)
+                nc.vector.scalar_tensor_tensor(
+                    out=o[:].rearrange("f n p -> f (n p)"),
+                    in0=rinv[:],
+                    scalar=1.0e12,
+                    in1=codes[(g, h)][:],
+                    op0=ALU.min,
+                    op1=ALU.mult,
+                )
+                nc.sync.dma_start(
+                    out=out[g * NB : (g + 1) * NB, h * P : (h + 1) * P, :].rearrange("n f p -> f n p"),
+                    in_=o[:, :, 0 : T - 1],
+                )
+
+        prep_x(0)
+        ps_b = aux.tile([P, P], BF16, name="ps_b", tag="aux")
+        nc.tensor.transpose(ps_b[:], bias_rows[:], ident_bf[:])
+        nc.vector.tensor_copy(out=bias_sb[:], in_=ps_b[:, 0:6])
+        prep_w(0)
+        prep_w(1)
+        prep_x(1)
+        for g in range(G):
+            mx(g, 0)
+            if g >= 2:
+                norm_b(g - 2)
+            mx(g, 1)
+            if g + 2 < G:
+                prep_x(g + 2)
+            norm_a(g)
+        norm_b(G - 2)
+        norm_b(G - 1)

@@ -21,8 +21,10 @@ PH = T // L
 BLK = NB * PH
 HALO = 4
 NCOL = (L + HALO) * BLK
+GC = NB * T
 UNIT0 = {4: 0, 3: 4, 2: 7}
 BIAS_COL = {4: 0, 3: 2, 2: 4}
+QUANT_RUNS = {4: ((0, 4),), 3: ((0, 2), (2, 1)), 2: ((0, 2),)}
 FLOPS = 2 * B * D * F * (2 * 127 + 3 * 126 + 4 * 125)
 
 
@@ -37,10 +39,37 @@ def tile_textheading_pa_t_kernel(tc, words_emb, W2, b2, W3, b3, W4, b4, out):
         xg = ctx.enter_context(tc.tile_pool(name="xg", bufs=2))
         code_pool = ctx.enter_context(tc.tile_pool(name="code", bufs=4))
         work = ctx.enter_context(tc.tile_pool(name="work", bufs=2))
-        split = ctx.enter_context(tc.tile_pool(name="split", bufs=4))
+        split = ctx.enter_context(tc.tile_pool(name="split", bufs=3))
         outp = ctx.enter_context(tc.tile_pool(name="outp", bufs=3))
         mxp = ctx.enter_context(tc.psum_pool(name="mxp", bufs=2))
         aux = ctx.enter_context(tc.psum_pool(name="aux", bufs=2))
+        ctx.enter_context(tc.manual_schedule())
+
+        bias_rows = const.tile([P, P], BF16, name="bias_rows")
+        nc.vector.memset(bias_rows[:], 0.0)
+        for K in WIDTHS:
+            c = BIAS_COL[K]
+            nc.scalar.dma_start(out=bias_rows[c : c + 2, :], in_=b_dram[K].rearrange("(h f) -> h f", h=2))
+        x_raw = {}
+        w_raw = {}
+
+        def load_x(g):
+            t = raw.tile([P, NB, D], BF16, name="x_raw%d" % g)
+            nc.sync.dma_start(out=t[:], in_=words_emb[g * NB : (g + 1) * NB].rearrange("n p d -> p n d"))
+            x_raw[g] = t
+
+        def load_w(h):
+            for K in WIDTHS:
+                t = raw.tile([P, K * D], BF16, name="w_raw%d_%d" % (K, h))
+                nc.sync.dma_start(out=t[:], in_=w_dram[K][h * P : (h + 1) * P].rearrange("f k d -> f (k d)"))
+                w_raw[(K, h)] = t
+
+        load_x(0)
+        load_w(0)
+        load_x(1)
+        load_w(1)
+        for g in range(2, G):
+            load_x(g)
 
         one_col = const.tile([P, 1], F32, name="one_col")
         nc.vector.memset(one_col[:], 1.0)
@@ -52,46 +81,17 @@ def tile_textheading_pa_t_kernel(tc, words_emb, W2, b2, W3, b3, W4, b4, out):
         nc.vector.tensor_copy(out=ident_bf[:], in_=ident[:])
         ones_bf = const.tile([P, P], BF16, name="ones_bf")
         nc.vector.memset(ones_bf[:], 1.0)
-        bias_rows = const.tile([P, P], BF16, name="bias_rows")
-        nc.vector.memset(bias_rows[:], 0.0)
+        ones_f32 = const.tile([P, P], F32, name="ones_f32")
+        nc.vector.memset(ones_f32[:], 1.0)
         halos = []
         for i in range(2):
             halo = const.tile([P, HALO * BLK * 4], BF16, name="halo%d" % i, align_bytes=64)
             nc.vector.memset(halo[:], 0.0)
             halos.append(halo)
 
-        for K in WIDTHS:
-            c = BIAS_COL[K]
-            nc.scalar.dma_start(out=bias_rows[c : c + 2, :], in_=b_dram[K].rearrange("(h f) -> h f", h=2))
-        x_raw = []
-        w_raw = {}
-
-        def load_x(g):
-            t = raw.tile([P, NB, D], BF16, name="x_raw%d" % g)
-            nc.sync.dma_start(out=t[:], in_=words_emb[g * NB : (g + 1) * NB].rearrange("n p d -> p n d"))
-            x_raw.append(t)
-
-        load_x(0)
-        for h in range(2):
-            for K in WIDTHS:
-                t = raw.tile([P, K * D], BF16, name="w_raw%d_%d" % (K, h))
-                nc.sync.dma_start(out=t[:], in_=w_dram[K][h * P : (h + 1) * P].rearrange("f k d -> f (k d)"))
-                w_raw[(K, h)] = t
-        for g in range(1, G):
-            load_x(g)
-
         w_codes = const.tile([P, 18 * P], U32, name="w_codes", align_bytes=64)
         w_scales = const.tile([P, 18 * P], U8, name="w_scales", align_bytes=64)
         bias_sb = const.tile([P, 6], F32, name="bias_sb")
-
-        flip = [0]
-
-        def copy_out(out_ap, in_ap):
-            if flip[0] % 2 == 0:
-                nc.scalar.copy(out=out_ap, in_=in_ap)
-            else:
-                nc.vector.tensor_copy(out=out_ap, in_=in_ap)
-            flip[0] += 1
 
         bank_tags = ["c4", "c3", "c2"]
         bank_no = [0]
@@ -104,17 +104,18 @@ def tile_textheading_pa_t_kernel(tc, words_emb, W2, b2, W3, b3, W4, b4, out):
                 for k0 in range(0, K, 2):
                     cnt = min(2, K - k0)
                     ps = mxp.tile([P, 4, P], F32, name="ps_w", tag=bank_tags[bank_no[0] % 3])
-                    bank_no[0] += 1
                     for i in range(cnt):
                         for u in range(2):
                             col = (k0 + i) * 256 + u * P
                             nc.tensor.transpose(ps[:, 2 * i + u, :], words[:, col : col + P], ident[:])
-                    copy_out(
-                        grp_w[:, k0 : k0 + cnt],
-                        ps[:, 0 : 2 * cnt, :].rearrange("q (c u) f -> q c f u", u=2),
-                    )
+                    src = ps[:, 0 : 2 * cnt, :].rearrange("q (c u) f -> q c f u", u=2)
+                    if k0 == 0:
+                        nc.scalar.copy(out=grp_w[:, k0 : k0 + cnt], in_=src)
+                    else:
+                        nc.vector.tensor_copy(out=grp_w[:, k0 : k0 + cnt], in_=src)
+                    bank_no[0] += 1
                 unit = h * 9 + UNIT0[K]
-                for k0, cnt in {4: ((0, 4),), 3: ((0, 2), (2, 1)), 2: ((0, 2),)}[K]:
+                for k0, cnt in QUANT_RUNS[K]:
                     cols = slice((unit + k0) * P, (unit + k0 + cnt) * P)
                     nc.vector.quantize_mx(
                         out=w_codes[:, cols].bitcast(FP8X4),
@@ -122,121 +123,238 @@ def tile_textheading_pa_t_kernel(tc, words_emb, W2, b2, W3, b3, W4, b4, out):
                         in_=grp[:, k0 * D : (k0 + cnt) * D],
                     )
 
+        ps_x = {}
+        x_grp = {}
         x_codes = {}
         x_scales = {}
 
-        def prep_x(g):
+        def transposes_x(g):
             words = x_raw[g][:].bitcast(F32)
-            grp = xg.tile([P, L * BLK * 4], BF16, name="x_grp", align_bytes=64)
-            grp_w = grp[:].bitcast(F32)
-            grp_v = grp_w.rearrange("q (pl n ph u) -> q pl n ph u", pl=L, n=NB, ph=PH, u=2)
+            banks = []
             for n0 in range(0, NB, 2):
                 ps = aux.tile([P, 4, P], F32, name="ps_x", tag="aux")
                 for i in range(2):
                     for u in range(2):
                         nc.tensor.transpose(ps[:, 2 * i + u, :], words[:, n0 + i, u * P : (u + 1) * P], ident[:])
-                for i in range(2):
-                    nc.scalar.copy(
-                        out=grp_v[:, :, n0 + i, :, :],
-                        in_=ps[:, 2 * i : 2 * i + 2, :].rearrange("q u (ph pl) -> q pl ph u", pl=L),
-                    )
-            halo = halos[g % 2]
+                banks.append(ps)
+            ps_x[g] = banks
+
+        def evac_x(g):
+            grp = xg.tile([P, L * BLK * 4], BF16, name="x_grp", align_bytes=64)
+            grp_v = grp[:].bitcast(F32).rearrange("q (pl n ph u) -> q pl n ph u", pl=L, n=NB, ph=PH, u=2)
+            for n in range(NB):
+                i = n % 2
+                nc.scalar.copy(
+                    out=grp_v[:, :, n, :, :],
+                    in_=ps_x[g][n // 2][:, 2 * i : 2 * i + 2, :].rearrange("q u (ph pl) -> q pl ph u", pl=L),
+                )
+            x_grp[g] = grp
+            x_codes[g] = xq.tile([P, NCOL], U32, name="x_codes", align_bytes=64)
+            x_scales[g] = xq.tile([P, NCOL], U8, name="x_scales", align_bytes=64)
+
+        def quant_x_main(g):
+            nc.vector.quantize_mx(
+                out=x_codes[g][:, 0 : L * BLK].bitcast(FP8X4), scales=x_scales[g][:, 0 : L * BLK], in_=x_grp[g][:]
+            )
+
+        def halo_copy(g):
             rows = 3 * NB
             nc.vector.tensor_copy(
-                out=halo[:].bitcast(F32).rearrange("q (r w) -> q r w", w=2 * PH)[:, 0:rows, 0 : 2 * PH - 2],
-                in_=grp_w.rearrange("q (r w) -> q r w", w=2 * PH)[:, 0:rows, 2 : 2 * PH],
+                out=halos[g % 2][:].bitcast(F32).rearrange("q (r w) -> q r w", w=2 * PH)[:, 0:rows, 0 : 2 * PH - 2],
+                in_=x_grp[g][:].bitcast(F32).rearrange("q (r w) -> q r w", w=2 * PH)[:, 0:rows, 2 : 2 * PH],
             )
-            xc = xq.tile([P, NCOL], U32, name="x_codes", align_bytes=64)
-            xs = xq.tile([P, NCOL], U8, name="x_scales", align_bytes=64)
-            nc.vector.quantize_mx(out=xc[:, 0 : L * BLK].bitcast(FP8X4), scales=xs[:, 0 : L * BLK], in_=grp[:])
-            nc.vector.quantize_mx(out=xc[:, L * BLK : NCOL].bitcast(FP8X4), scales=xs[:, L * BLK : NCOL], in_=halo[:])
-            x_codes[g] = xc
-            x_scales[g] = xs
 
+        def quant_x_halo(g):
+            nc.vector.quantize_mx(
+                out=x_codes[g][:, L * BLK : NCOL].bitcast(FP8X4),
+                scales=x_scales[g][:, L * BLK : NCOL],
+                in_=halos[g % 2][:],
+            )
+
+        accs = {}
         codes = {}
 
-        def mx(g, h):
-            xc = x_codes[g]
-            xs = x_scales[g]
-            code = code_pool.tile([P, NB * T], F32, name="code%d" % h)
-            code_v = code[:].rearrange("f (m pl) -> f m pl", pl=L)
-            code_p = code[:].rearrange("f (n p) -> f n p", p=T)
-            for K in WIDTHS:
-                acc = mxp.tile([P, 512], F32, name="acc", tag="c%d" % K)
-                for k in range(K):
-                    unit = h * 9 + UNIT0[K] + k
-                    nc.tensor.matmul_mx(
-                        out=acc[:],
-                        lhsT=w_codes[:, unit * P : (unit + 1) * P].bitcast(FP8X4),
-                        lhsT_scale=w_scales[:, unit * P : (unit + 1) * P],
-                        rhs=xc[:, k * BLK : k * BLK + 512].bitcast(FP8X4),
-                        rhs_scale=xs[:, k * BLK : k * BLK + 512],
-                        start=(k == 0),
-                        stop=(k == K - 1),
-                    )
-                acc_v = acc[:].rearrange("f (pl m) -> f m pl", pl=L)
-                bias = bias_sb[:, BIAS_COL[K] + h : BIAS_COL[K] + h + 1]
-                if K == 4:
-                    nc.scalar.activation(out=code_v, in_=acc_v, func=ACT.Relu, bias=bias)
-                else:
-                    nc.vector.memset(code_p[:, :, T - K : T], 0.0)
-                    nc.vector.scalar_tensor_tensor(
-                        out=code_v, in0=acc_v, scalar=bias, in1=code_v, op0=ALU.add, op1=ALU.max
-                    )
+        def passes(g, h, K):
+            acc = mxp.tile([P, 512], F32, name="acc", tag="c%d" % K)
+            for k in range(K):
+                unit = h * 9 + UNIT0[K] + k
+                nc.tensor.matmul_mx(
+                    out=acc[:],
+                    lhsT=w_codes[:, unit * P : (unit + 1) * P].bitcast(FP8X4),
+                    lhsT_scale=w_scales[:, unit * P : (unit + 1) * P],
+                    rhs=x_codes[g][:, k * BLK : k * BLK + 512].bitcast(FP8X4),
+                    rhs_scale=x_scales[g][:, k * BLK : k * BLK + 512],
+                    start=(k == 0),
+                    stop=(k == K - 1),
+                )
+            accs[(g, h, K)] = acc
+
+        def relu4(g, h):
+            code = code_pool.tile([P, GC], F32, name="code%d" % h)
             codes[(g, h)] = code
+            nc.scalar.activation(
+                out=code[:].rearrange("f (m pl) -> f m pl", pl=L),
+                in_=accs[(g, h, 4)][:].rearrange("f (pl m) -> f m pl", pl=L),
+                func=ACT.Relu,
+                bias=bias_sb[:, BIAS_COL[4] + h : BIAS_COL[4] + h + 1],
+            )
 
-        parts = {}
-
-        def norm_a(g):
-            sq = []
-            for h in range(2):
-                s = work.tile([P, NB * T], F32, name="sq%d" % h)
-                nc.scalar.activation(out=s[:], in_=codes[(g, h)][:], func=ACT.Square)
-                sq.append(s)
-            tot = work.tile([P, NB * T], F32, name="tot")
-            nc.gpsimd.tensor_tensor(out=tot[:], in0=sq[0][:], in1=sq[1][:], op=ALU.add)
-            hi = split.tile([P, NB * T], BF16, name="hi")
-            nc.scalar.copy(out=hi[:], in_=tot[:])
-            lo = split.tile([P, NB * T], BF16, name="lo")
-            nc.gpsimd.tensor_tensor(out=lo[:], in0=tot[:], in1=hi[:], op=ALU.subtract)
-            parts[g] = (hi, lo)
-
-        def norm_b(g):
-            hi, lo = parts[g]
-            ss = aux.tile([P, NB * T], F32, name="ss", tag="aux")
-            nc.tensor.matmul(out=ss[:], lhsT=ones_bf[:], rhs=hi[:], start=True, stop=False)
-            nc.tensor.matmul(out=ss[:], lhsT=ones_bf[:], rhs=lo[:], start=False, stop=True)
-            rinv = work.tile([P, NB * T], F32, name="rinv")
-            nc.scalar.activation(out=rinv[:], in_=ss[:], func=ACT.Abs_reciprocal_sqrt)
-            for h in range(2):
-                o = outp.tile([P, NB, T], F32, name="o%d" % h)
+        def merge(g, h, K, pieces=1):
+            code = codes[(g, h)]
+            nc.vector.memset(code[:].rearrange("f (n p) -> f n p", p=T)[:, :, T - K : T], 0.0)
+            code_v = code[:].rearrange("f (m pl) -> f m pl", pl=L)
+            acc_v = accs[(g, h, K)][:].rearrange("f (pl m) -> f m pl", pl=L)
+            step = BLK // pieces
+            for c in range(pieces):
+                ms = slice(c * step, (c + 1) * step)
                 nc.vector.scalar_tensor_tensor(
-                    out=o[:].rearrange("f n p -> f (n p)"),
-                    in0=rinv[:],
-                    scalar=1.0e12,
-                    in1=codes[(g, h)][:],
-                    op0=ALU.min,
-                    op1=ALU.mult,
-                )
-                nc.sync.dma_start(
-                    out=out[g * NB : (g + 1) * NB, h * P : (h + 1) * P, :].rearrange("n f p -> f n p"),
-                    in_=o[:, :, 0 : T - 1],
+                    out=code_v[:, ms, :],
+                    in0=acc_v[:, ms, :],
+                    scalar=bias_sb[:, BIAS_COL[K] + h : BIAS_COL[K] + h + 1],
+                    in1=code_v[:, ms, :],
+                    op0=ALU.add,
+                    op1=ALU.max,
                 )
 
-        prep_x(0)
+        sqs = {}
+        tots = {}
+        his = {}
+        los = {}
+        rinvs = {}
+        sss = {}
+
+        def square(g, h, cs=slice(0, GC)):
+            if (g, h) not in sqs:
+                sqs[(g, h)] = work.tile([P, GC], F32, name="sq%d" % h)
+            nc.scalar.activation(out=sqs[(g, h)][:, cs], in_=codes[(g, h)][:, cs], func=ACT.Square)
+
+        def add_halves(g):
+            tots[g] = work.tile([P, GC], F32, name="tot")
+            nc.gpsimd.tensor_tensor(out=tots[g][:], in0=sqs[(g, 0)][:], in1=sqs[(g, 1)][:], op=ALU.add)
+
+        def high_part(g):
+            his[g] = split.tile([P, GC], BF16, name="hi")
+            nc.scalar.copy(out=his[g][:], in_=tots[g][:])
+
+        def low_part(g):
+            los[g] = split.tile([P, GC], BF16, name="lo")
+            nc.gpsimd.tensor_tensor(out=los[g][:], in0=tots[g][:], in1=his[g][:], op=ALU.subtract)
+
+        def sum_filters(g):
+            ss = aux.tile([P, GC], F32, name="ss", tag="aux")
+            nc.tensor.matmul(out=ss[:], lhsT=ones_bf[:], rhs=his[g][:], start=True, stop=False)
+            nc.tensor.matmul(out=ss[:], lhsT=ones_bf[:], rhs=los[g][:], start=False, stop=True)
+            sss[g] = ss
+
+        def rsqrt(g):
+            rinvs[g] = work.tile([P, GC], F32, name="rinv")
+            nc.scalar.activation(out=rinvs[g][:], in_=sss[g][:], func=ACT.Abs_reciprocal_sqrt)
+
+        def scale_store(g, h):
+            o = outp.tile([P, NB, T], F32, name="o%d" % h)
+            nc.vector.scalar_tensor_tensor(
+                out=o[:].rearrange("f n p -> f (n p)"),
+                in0=rinvs[g][:],
+                scalar=1.0e12,
+                in1=codes[(g, h)][:],
+                op0=ALU.min,
+                op1=ALU.mult,
+            )
+            nc.sync.dma_start(
+                out=out[g * NB : (g + 1) * NB, h * P : (h + 1) * P, :].rearrange("n f p -> f n p"),
+                in_=o[:, :, 0 : T - 1],
+            )
+
+        transposes_x(0)
+        evac_x(0)
+        quant_x_main(0)
+        halo_copy(0)
         ps_b = aux.tile([P, P], BF16, name="ps_b", tag="aux")
         nc.tensor.transpose(ps_b[:], bias_rows[:], ident_bf[:])
         nc.vector.tensor_copy(out=bias_sb[:], in_=ps_b[:, 0:6])
+        quant_x_halo(0)
         prep_w(0)
-        prep_w(1)
-        prep_x(1)
+
         for g in range(G):
-            mx(g, 0)
+            ahead = g >= 1 and g + 1 < G
+            passes(g, 0, 4)
+            if ahead:
+                evac_x(g + 1)
+            passes(g, 0, 3)
+            passes(g, 0, 2)
+            relu4(g, 0)
+            if ahead:
+                quant_x_main(g + 1)
+                halo_copy(g + 1)
+            if g >= 1:
+                square(g - 1, 1)
+                add_halves(g - 1)
+            merge(g, 0, 3)
+            if ahead:
+                quant_x_halo(g + 1)
+            merge(g, 0, 2)
+            if g == 0:
+                transposes_x(1)
+                evac_x(1)
+                prep_w(1)
+                quant_x_main(1)
+                halo_copy(1)
             if g >= 2:
-                norm_b(g - 2)
-            mx(g, 1)
+                sum_filters(g - 2)
+                rsqrt(g - 2)
+            passes(g, 1, 4)
+            passes(g, 1, 3)
+            passes(g, 1, 2)
+            if g >= 1:
+                high_part(g - 1)
+                low_part(g - 1)
+            if g >= 2:
+                scale_store(g - 2, 0)
+                scale_store(g - 2, 1)
+            relu4(g, 1)
+            square(g, 0)
+            merge(g, 1, 3)
+            if g == 0:
+                quant_x_halo(1)
+            merge(g, 1, 2, pieces=(2 if g == G - 1 else 1))
             if g + 2 < G:
-                prep_x(g + 2)
-            norm_a(g)
-        norm_b(G - 2)
-        norm_b(G - 1)
+                transposes_x(g + 2)
+
+        sum_filters(G - 2)
+        rsqrt(G - 2)
+        g = G - 1
+        half = GC // 2
+        last_ss = []
+        for c in range(2):
+            ss = aux.tile([P, half], F32, name="ss_last", tag="aux")
+            nc.tensor.matmul(
+                out=ss[:], lhsT=ones_f32[:], rhs=sqs[(g, 0)][:, c * half : (c + 1) * half], start=True, stop=False
+            )
+            last_ss.append(ss)
+        for c in range(2):
+            square(g, 1, slice(c * half, (c + 1) * half))
+        scale_store(G - 2, 0)
+        scale_store(G - 2, 1)
+        rinv = work.tile([P, GC], F32, name="rinv")
+        for c in range(2):
+            cs = slice(c * half, (c + 1) * half)
+            nc.tensor.matmul(out=last_ss[c][:], lhsT=ones_f32[:], rhs=sqs[(g, 1)][:, cs], start=False, stop=True)
+            nc.scalar.activation(out=rinv[:, cs], in_=last_ss[c][:], func=ACT.Abs_reciprocal_sqrt)
+        for c in range(2):
+            cs = slice(c * half, (c + 1) * half)
+            for h in range(2):
+                o = outp.tile([P, NB // 2, T], F32, name="o_last%d" % h)
+                nc.vector.scalar_tensor_tensor(
+                    out=o[:].rearrange("f n p -> f (n p)"),
+                    in0=rinv[:, cs],
+                    scalar=1.0e12,
+                    in1=codes[(g, h)][:, cs],
+                    op0=ALU.min,
+                    op1=ALU.mult,
+                )
+                n0 = g * NB + c * (NB // 2)
+                queue = nc.sync if h == 0 else nc.scalar
+                queue.dma_start(
+                    out=out[n0 : n0 + NB // 2, h * P : (h + 1) * P, :].rearrange("n f p -> f n p"),
+                    in_=o[:, :, 0 : T - 1],
+                )

@@ -77,6 +77,10 @@ def tile_textheading_pa_t_kernel(tc, words_emb, W2, b2, W3, b3, W4, b4, out):
         nc.scalar.activation(out=dummy[:], in_=one_col[:], func=ACT.Abs_reciprocal_sqrt)
         ident = const.tile([P, P], F32, name="ident")
         make_identity(nc, ident[:])
+        perm = const.tile([P, P], F32, name="perm")
+        nc.vector.tensor_copy(
+            out=perm[:].rearrange("i (pl ph) -> i pl ph", pl=L), in_=ident[:].rearrange("i (ph pl) -> i pl ph", pl=L)
+        )
         ident_bf = const.tile([P, P], BF16, name="ident_bf")
         nc.vector.tensor_copy(out=ident_bf[:], in_=ident[:])
         ones_bf = const.tile([P, P], BF16, name="ones_bf")
@@ -135,7 +139,7 @@ def tile_textheading_pa_t_kernel(tc, words_emb, W2, b2, W3, b3, W4, b4, out):
                 ps = aux.tile([P, 4, P], F32, name="ps_x", tag="aux")
                 for i in range(2):
                     for u in range(2):
-                        nc.tensor.transpose(ps[:, 2 * i + u, :], words[:, n0 + i, u * P : (u + 1) * P], ident[:])
+                        nc.tensor.transpose(ps[:, 2 * i + u, :], words[:, n0 + i, u * P : (u + 1) * P], perm[:])
                 banks.append(ps)
             ps_x[g] = banks
 
@@ -146,7 +150,7 @@ def tile_textheading_pa_t_kernel(tc, words_emb, W2, b2, W3, b3, W4, b4, out):
                 i = n % 2
                 nc.scalar.copy(
                     out=grp_v[:, :, n, :, :],
-                    in_=ps_x[g][n // 2][:, 2 * i : 2 * i + 2, :].rearrange("q u (ph pl) -> q pl ph u", pl=L),
+                    in_=ps_x[g][n // 2][:, 2 * i : 2 * i + 2, :].rearrange("q u (pl ph) -> q pl ph u", pl=L),
                 )
             x_grp[g] = grp
             x_codes[g] = xq.tile([P, NCOL], U32, name="x_codes", align_bytes=64)
@@ -193,8 +197,8 @@ def tile_textheading_pa_t_kernel(tc, words_emb, W2, b2, W3, b3, W4, b4, out):
             code = code_pool.tile([P, GC], F32, name="code%d" % h)
             codes[(g, h)] = code
             nc.scalar.activation(
-                out=code[:].rearrange("f (m pl) -> f m pl", pl=L),
-                in_=accs[(g, h, 4)][:].rearrange("f (pl m) -> f m pl", pl=L),
+                out=code[:].rearrange("f (m a b) -> f a m b", a=L // 4, b=4),
+                in_=accs[(g, h, 4)][:].rearrange("f (a b m) -> f a m b", a=L // 4, b=4),
                 func=ACT.Relu,
                 bias=bias_sb[:, BIAS_COL[4] + h : BIAS_COL[4] + h + 1],
             )
@@ -207,14 +211,15 @@ def tile_textheading_pa_t_kernel(tc, words_emb, W2, b2, W3, b3, W4, b4, out):
             step = BLK // pieces
             for c in range(pieces):
                 ms = slice(c * step, (c + 1) * step)
-                nc.vector.scalar_tensor_tensor(
-                    out=code_v[:, ms, :],
-                    in0=acc_v[:, ms, :],
-                    scalar=bias_sb[:, BIAS_COL[K] + h : BIAS_COL[K] + h + 1],
-                    in1=code_v[:, ms, :],
-                    op0=ALU.add,
-                    op1=ALU.max,
-                )
+                for a in range(0, L, 4):
+                    nc.vector.scalar_tensor_tensor(
+                        out=code_v[:, ms, a : a + 4],
+                        in0=acc_v[:, ms, a : a + 4],
+                        scalar=bias_sb[:, BIAS_COL[K] + h : BIAS_COL[K] + h + 1],
+                        in1=code_v[:, ms, a : a + 4],
+                        op0=ALU.add,
+                        op1=ALU.max,
+                    )
 
         sqs = {}
         tots = {}

@@ -14,14 +14,11 @@ ALU = mybir.AluOpType
 P = 128
 B, T, D, F = 32, 128, 512, 256
 WIDTHS = (4, 3, 2)
-NB = 4
-G = B // NB
+SIZES = (8, 8, 8, 4, 4)
 L = 8
 PH = T // L
-BLK = NB * PH
-HALO = 4
-NCOL = (L + HALO) * BLK
-GC = NB * T
+NW = B // 4
+WC = 512
 UNIT0 = {4: 0, 3: 4, 2: 7}
 BIAS_COL = {4: 0, 3: 2, 2: 4}
 QUANT_RUNS = {4: ((0, 4),), 3: ((0, 2), (2, 1)), 2: ((0, 2),)}
@@ -32,6 +29,8 @@ def tile_textheading_pa_t_kernel(tc, words_emb, W2, b2, W3, b3, W4, b4, out):
     nc = tc.nc
     w_dram = {2: W2, 3: W3, 4: W4}
     b_dram = {2: b2, 3: b3, 4: b4}
+    win = [(g, a) for g, nb in enumerate(SIZES) for a in range(nb // 4)]
+    first_batch = [sum(SIZES[:g]) for g in range(len(SIZES))]
     with ExitStack() as ctx:
         const = ctx.enter_context(tc.tile_pool(name="const", bufs=1))
         raw = ctx.enter_context(tc.tile_pool(name="raw", bufs=1))
@@ -53,10 +52,10 @@ def tile_textheading_pa_t_kernel(tc, words_emb, W2, b2, W3, b3, W4, b4, out):
         x_raw = {}
         w_raw = {}
 
-        def load_x(g):
-            t = raw.tile([P, NB, D], BF16, name="x_raw%d" % g)
-            nc.sync.dma_start(out=t[:], in_=words_emb[g * NB : (g + 1) * NB].rearrange("n p d -> p n d"))
-            x_raw[g] = t
+        def load_x(i):
+            t = raw.tile([P, 4, D], BF16, name="x_raw%d" % i)
+            nc.sync.dma_start(out=t[:], in_=words_emb[4 * i : 4 * i + 4].rearrange("n p d -> p n d"))
+            x_raw[i] = t
 
         def load_w(h):
             for K in WIDTHS:
@@ -65,11 +64,11 @@ def tile_textheading_pa_t_kernel(tc, words_emb, W2, b2, W3, b3, W4, b4, out):
                 w_raw[(K, h)] = t
 
         load_x(0)
-        load_w(0)
         load_x(1)
+        load_w(0)
         load_w(1)
-        for g in range(2, G):
-            load_x(g)
+        for i in range(2, NW):
+            load_x(i)
 
         one_col = const.tile([P, 1], F32, name="one_col")
         nc.vector.memset(one_col[:], 1.0)
@@ -87,11 +86,12 @@ def tile_textheading_pa_t_kernel(tc, words_emb, W2, b2, W3, b3, W4, b4, out):
         nc.vector.memset(ones_bf[:], 1.0)
         ones_f32 = const.tile([P, P], F32, name="ones_f32")
         nc.vector.memset(ones_f32[:], 1.0)
-        halos = []
-        for i in range(2):
-            halo = const.tile([P, HALO * BLK * 4], BF16, name="halo%d" % i, align_bytes=64)
-            nc.vector.memset(halo[:], 0.0)
-            halos.append(halo)
+        halos = {}
+        for nb in (8, 4):
+            for i in range(2):
+                halo = const.tile([P, 4 * nb * PH * 4], BF16, name="halo%d_%d" % (nb, i), align_bytes=64)
+                nc.vector.memset(halo[:], 0.0)
+                halos[(nb, i)] = halo
 
         w_codes = const.tile([P, 18 * P], U32, name="w_codes", align_bytes=64)
         w_scales = const.tile([P, 18 * P], U8, name="w_scales", align_bytes=64)
@@ -132,94 +132,124 @@ def tile_textheading_pa_t_kernel(tc, words_emb, W2, b2, W3, b3, W4, b4, out):
         x_codes = {}
         x_scales = {}
 
-        def transposes_x(g):
-            words = x_raw[g][:].bitcast(F32)
+        def transposes_x(i):
+            words = x_raw[i][:].bitcast(F32)
             banks = []
-            for n0 in range(0, NB, 2):
+            for n0 in range(0, 4, 2):
                 ps = aux.tile([P, 4, P], F32, name="ps_x", tag="aux")
-                for i in range(2):
+                for j in range(2):
                     for u in range(2):
-                        nc.tensor.transpose(ps[:, 2 * i + u, :], words[:, n0 + i, u * P : (u + 1) * P], perm[:])
+                        nc.tensor.transpose(ps[:, 2 * j + u, :], words[:, n0 + j, u * P : (u + 1) * P], perm[:])
                 banks.append(ps)
-            ps_x[g] = banks
+            ps_x[i] = banks
 
-        def evac_x(g):
-            grp = xg.tile([P, L * BLK * 4], BF16, name="x_grp", align_bytes=64)
-            grp_v = grp[:].bitcast(F32).rearrange("q (pl n ph u) -> q pl n ph u", pl=L, n=NB, ph=PH, u=2)
-            for n in range(NB):
-                i = n % 2
-                nc.scalar.copy(
-                    out=grp_v[:, :, n, :, :],
-                    in_=ps_x[g][n // 2][:, 2 * i : 2 * i + 2, :].rearrange("q u (pl ph) -> q pl ph u", pl=L),
-                )
-            x_grp[g] = grp
-            x_codes[g] = xq.tile([P, NCOL], U32, name="x_codes", align_bytes=64)
-            x_scales[g] = xq.tile([P, NCOL], U8, name="x_scales", align_bytes=64)
+        def evac_x(i, both=False):
+            g, part = win[i]
+            nb = SIZES[g]
+            if part == 0:
+                x_grp[g] = xg.tile([P, L * nb * PH * 4], BF16, name="x_grp", align_bytes=64)
+                x_codes[g] = xq.tile([P, 12 * nb * PH], U32, name="x_codes", align_bytes=64)
+                x_scales[g] = xq.tile([P, 12 * nb * PH], U8, name="x_scales", align_bytes=64)
+            grp_v = x_grp[g][:].bitcast(F32).rearrange("q (pl n ph u) -> q pl n ph u", pl=L, n=nb, ph=PH, u=2)
+            for n in range(4):
+                j = n % 2
+                dst = grp_v[:, :, 4 * part + n, :, :]
+                src = ps_x[i][n // 2][:, 2 * j : 2 * j + 2, :].rearrange("q u (pl ph) -> q pl ph u", pl=L)
+                if both and n >= 2:
+                    nc.vector.tensor_copy(out=dst, in_=src)
+                else:
+                    nc.scalar.copy(out=dst, in_=src)
 
         def quant_x_main(g):
+            cols = L * SIZES[g] * PH
             nc.vector.quantize_mx(
-                out=x_codes[g][:, 0 : L * BLK].bitcast(FP8X4), scales=x_scales[g][:, 0 : L * BLK], in_=x_grp[g][:]
+                out=x_codes[g][:, 0:cols].bitcast(FP8X4), scales=x_scales[g][:, 0:cols], in_=x_grp[g][:]
             )
 
         def halo_copy(g):
-            rows = 3 * NB
-            nc.vector.tensor_copy(
-                out=halos[g % 2][:].bitcast(F32).rearrange("q (r w) -> q r w", w=2 * PH)[:, 0:rows, 0 : 2 * PH - 2],
+            rows = 3 * SIZES[g]
+            nc.scalar.copy(
+                out=halos[(SIZES[g], g % 2)][:]
+                .bitcast(F32)
+                .rearrange("q (r w) -> q r w", w=2 * PH)[:, 0:rows, 0 : 2 * PH - 2],
                 in_=x_grp[g][:].bitcast(F32).rearrange("q (r w) -> q r w", w=2 * PH)[:, 0:rows, 2 : 2 * PH],
             )
 
         def quant_x_halo(g):
+            blk = SIZES[g] * PH
             nc.vector.quantize_mx(
-                out=x_codes[g][:, L * BLK : NCOL].bitcast(FP8X4),
-                scales=x_scales[g][:, L * BLK : NCOL],
-                in_=halos[g % 2][:],
+                out=x_codes[g][:, L * blk : 12 * blk].bitcast(FP8X4),
+                scales=x_scales[g][:, L * blk : 12 * blk],
+                in_=halos[(SIZES[g], g % 2)][:],
             )
 
         accs = {}
         codes = {}
 
-        def passes(g, h, K):
-            acc = mxp.tile([P, 512], F32, name="acc", tag="c%d" % K)
+        def passes(w, h, K):
+            g, a = win[w]
+            blk = SIZES[g] * PH
+            acc = mxp.tile([P, WC], F32, name="acc", tag="c%d" % K)
             for k in range(K):
                 unit = h * 9 + UNIT0[K] + k
+                c0 = (4 * a + k) * blk
                 nc.tensor.matmul_mx(
                     out=acc[:],
                     lhsT=w_codes[:, unit * P : (unit + 1) * P].bitcast(FP8X4),
                     lhsT_scale=w_scales[:, unit * P : (unit + 1) * P],
-                    rhs=x_codes[g][:, k * BLK : k * BLK + 512].bitcast(FP8X4),
-                    rhs_scale=x_scales[g][:, k * BLK : k * BLK + 512],
+                    rhs=x_codes[g][:, c0 : c0 + WC].bitcast(FP8X4),
+                    rhs_scale=x_scales[g][:, c0 : c0 + WC],
                     start=(k == 0),
                     stop=(k == K - 1),
                 )
-            accs[(g, h, K)] = acc
+            accs[(w, h, K)] = acc
 
-        def relu4(g, h):
-            code = code_pool.tile([P, GC], F32, name="code%d" % h)
-            codes[(g, h)] = code
+        def relu4(w, h):
+            g, a = win[w]
+            code = code_pool.tile([P, WC], F32, name="code%d" % h)
+            codes[(w, h)] = code
+            if SIZES[g] == 8:
+                dst = code[:].rearrange("f (m b) -> f m b", b=4)
+                src = accs[(w, h, 4)][:].rearrange("f (b m) -> f m b", b=4)
+            else:
+                dst = code[:].rearrange("f (m s b) -> f s m b", s=2, b=4)
+                src = accs[(w, h, 4)][:].rearrange("f (s b m) -> f s m b", s=2, b=4)
             nc.scalar.activation(
-                out=code[:].rearrange("f (m a b) -> f a m b", a=L // 4, b=4),
-                in_=accs[(g, h, 4)][:].rearrange("f (a b m) -> f a m b", a=L // 4, b=4),
-                func=ACT.Relu,
-                bias=bias_sb[:, BIAS_COL[4] + h : BIAS_COL[4] + h + 1],
+                out=dst, in_=src, func=ACT.Relu, bias=bias_sb[:, BIAS_COL[4] + h : BIAS_COL[4] + h + 1]
             )
 
-        def merge(g, h, K, pieces=1):
-            code = codes[(g, h)]
-            nc.vector.memset(code[:].rearrange("f (n p) -> f n p", p=T)[:, :, T - K : T], 0.0)
-            code_v = code[:].rearrange("f (m pl) -> f m pl", pl=L)
-            acc_v = accs[(g, h, K)][:].rearrange("f (pl m) -> f m pl", pl=L)
-            step = BLK // pieces
-            for c in range(pieces):
-                ms = slice(c * step, (c + 1) * step)
-                for a in range(0, L, 4):
-                    nc.vector.scalar_tensor_tensor(
-                        out=code_v[:, ms, a : a + 4],
-                        in0=acc_v[:, ms, a : a + 4],
-                        scalar=bias_sb[:, BIAS_COL[K] + h : BIAS_COL[K] + h + 1],
-                        in1=code_v[:, ms, a : a + 4],
-                        op0=ALU.add,
-                        op1=ALU.max,
+        def merge(w, h, K, pieces=1):
+            g, a = win[w]
+            code = codes[(w, h)]
+            acc = accs[(w, h, K)]
+            bias = bias_sb[:, BIAS_COL[K] + h : BIAS_COL[K] + h + 1]
+            pairs = []
+            if SIZES[g] == 8:
+                if a == 1:
+                    nc.vector.memset(
+                        code[:].rearrange("f (n ph b) -> f n ph b", ph=PH, b=4)[:, :, PH - 1, 4 - K : 4], 0.0
                     )
+                pairs.append((code[:].rearrange("f (m b) -> f m b", b=4), acc[:].rearrange("f (b m) -> f m b", b=4)))
+            else:
+                nc.vector.memset(code[:].rearrange("f (n p) -> f n p", p=T)[:, :, T - K : T], 0.0)
+                code_v = code[:].rearrange("f (m pl) -> f m pl", pl=L)
+                acc_v = acc[:].rearrange("f (pl m) -> f m pl", pl=L)
+                step = 64 // pieces
+                for c in range(pieces):
+                    ms = slice(c * step, (c + 1) * step)
+                    for s in range(0, L, 4):
+                        pairs.append((code_v[:, ms, s : s + 4], acc_v[:, ms, s : s + 4]))
+            for code_ap, acc_ap in pairs:
+                nc.vector.scalar_tensor_tensor(
+                    out=code_ap, in0=acc_ap, scalar=bias, in1=code_ap, op0=ALU.add, op1=ALU.max
+                )
+
+        def half(w, h):
+            for K in WIDTHS:
+                passes(w, h, K)
+            relu4(w, h)
+            merge(w, h, 3)
+            merge(w, h, 2)
 
         sqs = {}
         tots = {}
@@ -227,139 +257,165 @@ def tile_textheading_pa_t_kernel(tc, words_emb, W2, b2, W3, b3, W4, b4, out):
         los = {}
         rinvs = {}
         sss = {}
+        outs = {}
 
-        def square(g, h, cs=slice(0, GC)):
-            if (g, h) not in sqs:
-                sqs[(g, h)] = work.tile([P, GC], F32, name="sq%d" % h)
-            nc.scalar.activation(out=sqs[(g, h)][:, cs], in_=codes[(g, h)][:, cs], func=ACT.Square)
+        def square(w, h, cs=slice(0, WC)):
+            if (w, h) not in sqs:
+                sqs[(w, h)] = work.tile([P, WC], F32, name="sq%d" % h)
+            nc.scalar.activation(out=sqs[(w, h)][:, cs], in_=codes[(w, h)][:, cs], func=ACT.Square)
 
-        def add_halves(g):
-            tots[g] = work.tile([P, GC], F32, name="tot")
-            nc.gpsimd.tensor_tensor(out=tots[g][:], in0=sqs[(g, 0)][:], in1=sqs[(g, 1)][:], op=ALU.add)
+        def add_halves(w):
+            tots[w] = work.tile([P, WC], F32, name="tot")
+            nc.gpsimd.tensor_tensor(out=tots[w][:], in0=sqs[(w, 0)][:], in1=sqs[(w, 1)][:], op=ALU.add)
 
-        def high_part(g):
-            his[g] = split.tile([P, GC], BF16, name="hi")
-            nc.scalar.copy(out=his[g][:], in_=tots[g][:])
+        def high_part(w):
+            his[w] = split.tile([P, WC], BF16, name="hi")
+            nc.scalar.copy(out=his[w][:], in_=tots[w][:])
 
-        def low_part(g):
-            los[g] = split.tile([P, GC], BF16, name="lo")
-            nc.gpsimd.tensor_tensor(out=los[g][:], in0=tots[g][:], in1=his[g][:], op=ALU.subtract)
+        def low_part(w):
+            los[w] = split.tile([P, WC], BF16, name="lo")
+            nc.gpsimd.tensor_tensor(out=los[w][:], in0=tots[w][:], in1=his[w][:], op=ALU.subtract)
 
-        def sum_filters(g):
-            ss = aux.tile([P, GC], F32, name="ss", tag="aux")
-            nc.tensor.matmul(out=ss[:], lhsT=ones_bf[:], rhs=his[g][:], start=True, stop=False)
-            nc.tensor.matmul(out=ss[:], lhsT=ones_bf[:], rhs=los[g][:], start=False, stop=True)
-            sss[g] = ss
+        def sum_filters(w):
+            ss = aux.tile([P, WC], F32, name="ss", tag="aux")
+            nc.tensor.matmul(out=ss[:], lhsT=ones_bf[:], rhs=his[w][:], start=True, stop=False)
+            nc.tensor.matmul(out=ss[:], lhsT=ones_bf[:], rhs=los[w][:], start=False, stop=True)
+            sss[w] = ss
 
-        def rsqrt(g):
-            rinvs[g] = work.tile([P, GC], F32, name="rinv")
-            nc.scalar.activation(out=rinvs[g][:], in_=sss[g][:], func=ACT.Abs_reciprocal_sqrt)
+        def rsqrt(w):
+            rinvs[w] = work.tile([P, WC], F32, name="rinv")
+            nc.scalar.activation(out=rinvs[w][:], in_=sss[w][:], func=ACT.Abs_reciprocal_sqrt)
 
-        def scale_store(g, h):
-            o = outp.tile([P, NB, T], F32, name="o%d" % h)
-            nc.vector.scalar_tensor_tensor(
-                out=o[:].rearrange("f n p -> f (n p)"),
-                in0=rinvs[g][:],
-                scalar=1.0e12,
-                in1=codes[(g, h)][:],
-                op0=ALU.min,
-                op1=ALU.mult,
-            )
-            nc.sync.dma_start(
-                out=out[g * NB : (g + 1) * NB, h * P : (h + 1) * P, :].rearrange("n f p -> f n p"),
-                in_=o[:, :, 0 : T - 1],
-            )
+        def scale_store(w, h):
+            g, a = win[w]
+            nb = SIZES[g]
+            if a == 0:
+                outs[(g, h)] = outp.tile([P, nb, T], F32, name="o%d" % h)
+            o = outs[(g, h)]
+            if nb == 8:
+                dst = o[:].rearrange("f n (ph pl) -> f (n ph) pl", pl=L)[:, :, 4 * a : 4 * a + 4]
+                rin = rinvs[w][:].rearrange("f (m b) -> f m b", b=4)
+                cod = codes[(w, h)][:].rearrange("f (m b) -> f m b", b=4)
+            else:
+                dst = o[:].rearrange("f n p -> f (n p)")
+                rin = rinvs[w][:]
+                cod = codes[(w, h)][:]
+            nc.vector.scalar_tensor_tensor(out=dst, in0=rin, scalar=1.0e12, in1=cod, op0=ALU.min, op1=ALU.mult)
+            if a == nb // 4 - 1:
+                n0 = first_batch[g]
+                nc.sync.dma_start(
+                    out=out[n0 : n0 + nb, h * P : (h + 1) * P, :].rearrange("n f p -> f n p"),
+                    in_=o[:, :, 0 : T - 1],
+                )
 
         transposes_x(0)
-        evac_x(0)
+        evac_x(0, both=True)
+        transposes_x(1)
+        evac_x(1, both=True)
         quant_x_main(0)
         halo_copy(0)
         ps_b = aux.tile([P, P], BF16, name="ps_b", tag="aux")
         nc.tensor.transpose(ps_b[:], bias_rows[:], ident_bf[:])
         nc.vector.tensor_copy(out=bias_sb[:], in_=ps_b[:, 0:6])
-        quant_x_halo(0)
         prep_w(0)
+        quant_x_halo(0)
+        half(0, 0)
+        prep_w(1)
+        passes(1, 0, 4)
+        transposes_x(2)
+        evac_x(2)
+        passes(1, 0, 3)
+        passes(1, 0, 2)
+        relu4(1, 0)
+        merge(1, 0, 3)
+        merge(1, 0, 2)
+        square(0, 0)
+        transposes_x(3)
+        evac_x(3)
+        halo_copy(1)
+        square(1, 0)
+        quant_x_main(1)
+        half(0, 1)
+        quant_x_halo(1)
+        transposes_x(4)
+        evac_x(4)
+        square(0, 1)
+        add_halves(0)
+        high_part(0)
+        low_part(0)
+        half(1, 1)
+        transposes_x(5)
 
-        for g in range(G):
-            ahead = g >= 1 and g + 1 < G
-            passes(g, 0, 4)
+        for w in range(2, NW):
+            i = w + 3
+            ahead = i < NW
+            whole = ahead and win[i][1] == SIZES[win[i][0]] // 4 - 1
+            passes(w, 0, 4)
             if ahead:
-                evac_x(g + 1)
-            passes(g, 0, 3)
-            passes(g, 0, 2)
-            relu4(g, 0)
-            if ahead:
-                quant_x_main(g + 1)
-                halo_copy(g + 1)
-            if g >= 1:
-                square(g - 1, 1)
-                add_halves(g - 1)
-            merge(g, 0, 3)
-            if ahead:
-                quant_x_halo(g + 1)
-            merge(g, 0, 2)
-            if g == 0:
-                transposes_x(1)
-                evac_x(1)
-                prep_w(1)
-                quant_x_main(1)
-                halo_copy(1)
-            if g >= 2:
-                sum_filters(g - 2)
-                rsqrt(g - 2)
-            passes(g, 1, 4)
-            passes(g, 1, 3)
-            passes(g, 1, 2)
-            if g >= 1:
-                high_part(g - 1)
-                low_part(g - 1)
-            if g >= 2:
-                scale_store(g - 2, 0)
-                scale_store(g - 2, 1)
-            relu4(g, 1)
-            square(g, 0)
-            merge(g, 1, 3)
-            if g == 0:
-                quant_x_halo(1)
-            merge(g, 1, 2, pieces=(2 if g == G - 1 else 1))
-            if g + 2 < G:
-                transposes_x(g + 2)
+                evac_x(i)
+            passes(w, 0, 3)
+            passes(w, 0, 2)
+            relu4(w, 0)
+            if whole:
+                quant_x_main(win[i][0])
+                halo_copy(win[i][0])
+            square(w - 1, 1)
+            add_halves(w - 1)
+            merge(w, 0, 3)
+            if whole:
+                quant_x_halo(win[i][0])
+            merge(w, 0, 2)
+            sum_filters(w - 2)
+            rsqrt(w - 2)
+            passes(w, 1, 4)
+            passes(w, 1, 3)
+            passes(w, 1, 2)
+            high_part(w - 1)
+            low_part(w - 1)
+            scale_store(w - 2, 0)
+            scale_store(w - 2, 1)
+            relu4(w, 1)
+            square(w, 0)
+            merge(w, 1, 3)
+            merge(w, 1, 2, pieces=(2 if w == NW - 1 else 1))
+            if w + 4 < NW:
+                transposes_x(w + 4)
 
-        sum_filters(G - 2)
-        rsqrt(G - 2)
-        g = G - 1
-        half = GC // 2
+        sum_filters(NW - 2)
+        rsqrt(NW - 2)
+        w = NW - 1
+        piece = WC // 2
         last_ss = []
         for c in range(2):
-            ss = aux.tile([P, half], F32, name="ss_last", tag="aux")
+            ss = aux.tile([P, piece], F32, name="ss_last", tag="aux")
             nc.tensor.matmul(
-                out=ss[:], lhsT=ones_f32[:], rhs=sqs[(g, 0)][:, c * half : (c + 1) * half], start=True, stop=False
+                out=ss[:], lhsT=ones_f32[:], rhs=sqs[(w, 0)][:, c * piece : (c + 1) * piece], start=True, stop=False
             )
             last_ss.append(ss)
         for c in range(2):
-            square(g, 1, slice(c * half, (c + 1) * half))
-        scale_store(G - 2, 0)
-        scale_store(G - 2, 1)
-        rinv = work.tile([P, GC], F32, name="rinv")
+            square(w, 1, slice(c * piece, (c + 1) * piece))
+        scale_store(NW - 2, 0)
+        scale_store(NW - 2, 1)
+        rinv = work.tile([P, WC], F32, name="rinv")
         for c in range(2):
-            cs = slice(c * half, (c + 1) * half)
-            nc.tensor.matmul(out=last_ss[c][:], lhsT=ones_f32[:], rhs=sqs[(g, 1)][:, cs], start=False, stop=True)
+            cs = slice(c * piece, (c + 1) * piece)
+            nc.tensor.matmul(out=last_ss[c][:], lhsT=ones_f32[:], rhs=sqs[(w, 1)][:, cs], start=False, stop=True)
             nc.scalar.activation(out=rinv[:, cs], in_=last_ss[c][:], func=ACT.Abs_reciprocal_sqrt)
         for c in range(2):
-            cs = slice(c * half, (c + 1) * half)
+            cs = slice(c * piece, (c + 1) * piece)
             for h in range(2):
-                o = outp.tile([P, NB // 2, T], F32, name="o_last%d" % h)
+                o = outp.tile([P, 2, T], F32, name="o_last%d" % h)
                 nc.vector.scalar_tensor_tensor(
                     out=o[:].rearrange("f n p -> f (n p)"),
                     in0=rinv[:, cs],
                     scalar=1.0e12,
-                    in1=codes[(g, h)][:, cs],
+                    in1=codes[(w, h)][:, cs],
                     op0=ALU.min,
                     op1=ALU.mult,
                 )
-                n0 = g * NB + c * (NB // 2)
+                n0 = B - 4 + 2 * c
                 queue = nc.sync if h == 0 else nc.scalar
                 queue.dma_start(
-                    out=out[n0 : n0 + NB // 2, h * P : (h + 1) * P, :].rearrange("n f p -> f n p"),
+                    out=out[n0 : n0 + 2, h * P : (h + 1) * P, :].rearrange("n f p -> f n p"),
                     in_=o[:, :, 0 : T - 1],
                 )

@@ -14,11 +14,14 @@ ALU = mybir.AluOpType
 P = 128
 B, T, D, F = 32, 128, 512, 256
 WIDTHS = (4, 3, 2)
-SIZES = (8, 8, 8, 4, 4)
+NB = 4
+G = B // NB
 L = 8
 PH = T // L
-NW = B // 4
-WC = 512
+BLK = NB * PH
+HALO = 4
+NCOL = (L + HALO) * BLK
+GC = NB * T
 UNIT0 = {4: 0, 3: 4, 2: 7}
 BIAS_COL = {4: 0, 3: 2, 2: 4}
 QUANT_RUNS = {4: ((0, 4),), 3: ((0, 2), (2, 1)), 2: ((0, 2),)}
@@ -29,8 +32,6 @@ def tile_textheading_pa_t_kernel(tc, words_emb, W2, b2, W3, b3, W4, b4, out):
     nc = tc.nc
     w_dram = {2: W2, 3: W3, 4: W4}
     b_dram = {2: b2, 3: b3, 4: b4}
-    win = [(g, a) for g, nb in enumerate(SIZES) for a in range(nb // 4)]
-    first_batch = [sum(SIZES[:g]) for g in range(len(SIZES))]
     with ExitStack() as ctx:
         const = ctx.enter_context(tc.tile_pool(name="const", bufs=1))
         raw = ctx.enter_context(tc.tile_pool(name="raw", bufs=1))
@@ -38,7 +39,8 @@ def tile_textheading_pa_t_kernel(tc, words_emb, W2, b2, W3, b3, W4, b4, out):
         xg = ctx.enter_context(tc.tile_pool(name="xg", bufs=2))
         code_pool = ctx.enter_context(tc.tile_pool(name="code", bufs=4))
         work = ctx.enter_context(tc.tile_pool(name="work", bufs=2))
-        split = ctx.enter_context(tc.tile_pool(name="split", bufs=3))
+        split = ctx.enter_context(tc.tile_pool(name="split", bufs=2))
+        turn = ctx.enter_context(tc.tile_pool(name="turn", bufs=1))
         outp = ctx.enter_context(tc.tile_pool(name="outp", bufs=3))
         mxp = ctx.enter_context(tc.psum_pool(name="mxp", bufs=2))
         aux = ctx.enter_context(tc.psum_pool(name="aux", bufs=2))
@@ -52,10 +54,10 @@ def tile_textheading_pa_t_kernel(tc, words_emb, W2, b2, W3, b3, W4, b4, out):
         x_raw = {}
         w_raw = {}
 
-        def load_x(i):
-            t = raw.tile([P, 4, D], BF16, name="x_raw%d" % i)
-            nc.sync.dma_start(out=t[:], in_=words_emb[4 * i : 4 * i + 4].rearrange("n p d -> p n d"))
-            x_raw[i] = t
+        def load_x(g):
+            t = raw.tile([P, NB, D], BF16, name="x_raw%d" % g)
+            nc.sync.dma_start(out=t[:], in_=words_emb[g * NB : (g + 1) * NB].rearrange("n p d -> p n d"))
+            x_raw[g] = t
 
         def load_w(h):
             for K in WIDTHS:
@@ -64,11 +66,11 @@ def tile_textheading_pa_t_kernel(tc, words_emb, W2, b2, W3, b3, W4, b4, out):
                 w_raw[(K, h)] = t
 
         load_x(0)
-        load_x(1)
         load_w(0)
+        load_x(1)
         load_w(1)
-        for i in range(2, NW):
-            load_x(i)
+        for g in range(2, G):
+            load_x(g)
 
         one_col = const.tile([P, 1], F32, name="one_col")
         nc.vector.memset(one_col[:], 1.0)
@@ -86,12 +88,11 @@ def tile_textheading_pa_t_kernel(tc, words_emb, W2, b2, W3, b3, W4, b4, out):
         nc.vector.memset(ones_bf[:], 1.0)
         ones_f32 = const.tile([P, P], F32, name="ones_f32")
         nc.vector.memset(ones_f32[:], 1.0)
-        halos = {}
-        for nb in (8, 4):
-            for i in range(2):
-                halo = const.tile([P, 4 * nb * PH * 4], BF16, name="halo%d_%d" % (nb, i), align_bytes=64)
-                nc.vector.memset(halo[:], 0.0)
-                halos[(nb, i)] = halo
+        halos = []
+        for i in range(2):
+            halo = const.tile([P, HALO * BLK * 4], BF16, name="halo%d" % i, align_bytes=64)
+            nc.vector.memset(halo[:], 0.0)
+            halos.append(halo)
 
         w_codes = const.tile([P, 18 * P], U32, name="w_codes", align_bytes=64)
         w_scales = const.tile([P, 18 * P], U8, name="w_scales", align_bytes=64)
@@ -132,124 +133,103 @@ def tile_textheading_pa_t_kernel(tc, words_emb, W2, b2, W3, b3, W4, b4, out):
         x_codes = {}
         x_scales = {}
 
-        def transposes_x(i):
-            words = x_raw[i][:].bitcast(F32)
+        def transposes_x(g):
+            words = x_raw[g][:].bitcast(F32)
             banks = []
-            for n0 in range(0, 4, 2):
+            for n0 in range(0, NB, 2):
                 ps = aux.tile([P, 4, P], F32, name="ps_x", tag="aux")
-                for j in range(2):
+                for i in range(2):
                     for u in range(2):
-                        nc.tensor.transpose(ps[:, 2 * j + u, :], words[:, n0 + j, u * P : (u + 1) * P], perm[:])
+                        nc.tensor.transpose(ps[:, 2 * i + u, :], words[:, n0 + i, u * P : (u + 1) * P], perm[:])
                 banks.append(ps)
-            ps_x[i] = banks
+            ps_x[g] = banks
 
-        def evac_x(i, both=False):
-            g, part = win[i]
-            nb = SIZES[g]
-            if part == 0:
-                x_grp[g] = xg.tile([P, L * nb * PH * 4], BF16, name="x_grp", align_bytes=64)
-                x_codes[g] = xq.tile([P, 12 * nb * PH], U32, name="x_codes", align_bytes=64)
-                x_scales[g] = xq.tile([P, 12 * nb * PH], U8, name="x_scales", align_bytes=64)
-            grp_v = x_grp[g][:].bitcast(F32).rearrange("q (pl n ph u) -> q pl n ph u", pl=L, n=nb, ph=PH, u=2)
-            for n in range(4):
-                j = n % 2
-                dst = grp_v[:, :, 4 * part + n, :, :]
-                src = ps_x[i][n // 2][:, 2 * j : 2 * j + 2, :].rearrange("q u (pl ph) -> q pl ph u", pl=L)
-                if both and n >= 2:
-                    nc.vector.tensor_copy(out=dst, in_=src)
-                else:
-                    nc.scalar.copy(out=dst, in_=src)
+        def evac_x(g):
+            grp = xg.tile([P, L * BLK * 4], BF16, name="x_grp", align_bytes=64)
+            grp_v = grp[:].bitcast(F32).rearrange("q (pl n ph u) -> q pl n ph u", pl=L, n=NB, ph=PH, u=2)
+            for n in range(NB):
+                i = n % 2
+                nc.scalar.copy(
+                    out=grp_v[:, :, n, :, :],
+                    in_=ps_x[g][n // 2][:, 2 * i : 2 * i + 2, :].rearrange("q u (pl ph) -> q pl ph u", pl=L),
+                )
+            x_grp[g] = grp
+            x_codes[g] = xq.tile([P, NCOL], U32, name="x_codes", align_bytes=64)
+            x_scales[g] = xq.tile([P, NCOL], U8, name="x_scales", align_bytes=64)
 
         def quant_x_main(g):
-            cols = L * SIZES[g] * PH
             nc.vector.quantize_mx(
-                out=x_codes[g][:, 0:cols].bitcast(FP8X4), scales=x_scales[g][:, 0:cols], in_=x_grp[g][:]
+                out=x_codes[g][:, 0 : L * BLK].bitcast(FP8X4), scales=x_scales[g][:, 0 : L * BLK], in_=x_grp[g][:]
             )
 
         def halo_copy(g):
-            rows = 3 * SIZES[g]
+            rows = 3 * NB
             nc.scalar.copy(
-                out=halos[(SIZES[g], g % 2)][:]
-                .bitcast(F32)
-                .rearrange("q (r w) -> q r w", w=2 * PH)[:, 0:rows, 0 : 2 * PH - 2],
+                out=halos[g % 2][:].bitcast(F32).rearrange("q (r w) -> q r w", w=2 * PH)[:, 0:rows, 0 : 2 * PH - 2],
                 in_=x_grp[g][:].bitcast(F32).rearrange("q (r w) -> q r w", w=2 * PH)[:, 0:rows, 2 : 2 * PH],
             )
 
         def quant_x_halo(g):
-            blk = SIZES[g] * PH
             nc.vector.quantize_mx(
-                out=x_codes[g][:, L * blk : 12 * blk].bitcast(FP8X4),
-                scales=x_scales[g][:, L * blk : 12 * blk],
-                in_=halos[(SIZES[g], g % 2)][:],
+                out=x_codes[g][:, L * BLK : NCOL].bitcast(FP8X4),
+                scales=x_scales[g][:, L * BLK : NCOL],
+                in_=halos[g % 2][:],
             )
 
         accs = {}
         codes = {}
 
-        def passes(w, h, K):
-            g, a = win[w]
-            blk = SIZES[g] * PH
-            acc = mxp.tile([P, WC], F32, name="acc", tag="c%d" % K)
+        def passes(g, h, K):
+            acc = mxp.tile([P, 512], F32, name="acc", tag="c%d" % K)
             for k in range(K):
                 unit = h * 9 + UNIT0[K] + k
-                c0 = (4 * a + k) * blk
                 nc.tensor.matmul_mx(
                     out=acc[:],
                     lhsT=w_codes[:, unit * P : (unit + 1) * P].bitcast(FP8X4),
                     lhsT_scale=w_scales[:, unit * P : (unit + 1) * P],
-                    rhs=x_codes[g][:, c0 : c0 + WC].bitcast(FP8X4),
-                    rhs_scale=x_scales[g][:, c0 : c0 + WC],
+                    rhs=x_codes[g][:, k * BLK : k * BLK + 512].bitcast(FP8X4),
+                    rhs_scale=x_scales[g][:, k * BLK : k * BLK + 512],
                     start=(k == 0),
                     stop=(k == K - 1),
                 )
-            accs[(w, h, K)] = acc
+            accs[(g, h, K)] = acc
 
-        def relu4(w, h):
-            g, a = win[w]
-            code = code_pool.tile([P, WC], F32, name="code%d" % h)
-            codes[(w, h)] = code
-            if SIZES[g] == 8:
-                dst = code[:].rearrange("f (m b) -> f m b", b=4)
-                src = accs[(w, h, 4)][:].rearrange("f (b m) -> f m b", b=4)
-            else:
-                dst = code[:].rearrange("f (m s b) -> f s m b", s=2, b=4)
-                src = accs[(w, h, 4)][:].rearrange("f (s b m) -> f s m b", s=2, b=4)
+        def relu4(g, h):
+            code = code_pool.tile([P, GC], F32, name="code%d" % h)
+            codes[(g, h)] = code
             nc.scalar.activation(
-                out=dst, in_=src, func=ACT.Relu, bias=bias_sb[:, BIAS_COL[4] + h : BIAS_COL[4] + h + 1]
+                out=code[:].rearrange("f (m a b) -> f a m b", a=L // 4, b=4),
+                in_=accs[(g, h, 4)][:].rearrange("f (a b m) -> f a m b", a=L // 4, b=4),
+                func=ACT.Relu,
+                bias=bias_sb[:, BIAS_COL[4] + h : BIAS_COL[4] + h + 1],
             )
+            tail = code[:].rearrange("f (n p) -> f n p", p=T)[:, :, T - 3 : T]
+            nc.scalar.activation(out=tail, in_=tail, func=ACT.Relu, scale=-1.0)
 
-        def merge(w, h, K, pieces=1):
-            g, a = win[w]
-            code = codes[(w, h)]
-            acc = accs[(w, h, K)]
-            bias = bias_sb[:, BIAS_COL[K] + h : BIAS_COL[K] + h + 1]
-            pairs = []
-            if SIZES[g] == 8:
-                if a == 1:
-                    nc.vector.memset(
-                        code[:].rearrange("f (n ph b) -> f n ph b", ph=PH, b=4)[:, :, PH - 1, 4 - K : 4], 0.0
+        def merge(g, h, K, pieces=1):
+            code = codes[(g, h)]
+            code_v = code[:].rearrange("f (m pl) -> f m pl", pl=L)
+            acc_v = accs[(g, h, K)][:].rearrange("f (pl m) -> f m pl", pl=L)
+            step = BLK // pieces
+            for c in range(pieces):
+                ms = slice(c * step, (c + 1) * step)
+                for a in (4, 0) if K == 3 else (0, 4):
+                    nc.vector.scalar_tensor_tensor(
+                        out=code_v[:, ms, a : a + 4],
+                        in0=acc_v[:, ms, a : a + 4],
+                        scalar=bias_sb[:, BIAS_COL[K] + h : BIAS_COL[K] + h + 1],
+                        in1=code_v[:, ms, a : a + 4],
+                        op0=ALU.add,
+                        op1=ALU.max,
                     )
-                pairs.append((code[:].rearrange("f (m b) -> f m b", b=4), acc[:].rearrange("f (b m) -> f m b", b=4)))
-            else:
-                nc.vector.memset(code[:].rearrange("f (n p) -> f n p", p=T)[:, :, T - K : T], 0.0)
-                code_v = code[:].rearrange("f (m pl) -> f m pl", pl=L)
-                acc_v = acc[:].rearrange("f (pl m) -> f m pl", pl=L)
-                step = 64 // pieces
-                for c in range(pieces):
-                    ms = slice(c * step, (c + 1) * step)
-                    for s in range(0, L, 4):
-                        pairs.append((code_v[:, ms, s : s + 4], acc_v[:, ms, s : s + 4]))
-            for code_ap, acc_ap in pairs:
-                nc.vector.scalar_tensor_tensor(
-                    out=code_ap, in0=acc_ap, scalar=bias, in1=code_ap, op0=ALU.add, op1=ALU.max
-                )
 
-        def half(w, h):
-            for K in WIDTHS:
-                passes(w, h, K)
-            relu4(w, h)
-            merge(w, h, 3)
-            merge(w, h, 2)
+        def fix(g, h, ns=slice(0, NB)):
+            nc.scalar.activation(
+                out=codes[(g, h)][:].rearrange("f (n p) -> f n p", p=T)[:, ns, T - 2],
+                in_=accs[(g, h, 2)][:].rearrange("f (pl n ph) -> f pl n ph", pl=L, n=NB)[:, L - 2, ns, PH - 1],
+                func=ACT.Relu,
+                bias=bias_sb[:, BIAS_COL[2] + h : BIAS_COL[2] + h + 1],
+            )
 
         sqs = {}
         tots = {}
@@ -257,165 +237,149 @@ def tile_textheading_pa_t_kernel(tc, words_emb, W2, b2, W3, b3, W4, b4, out):
         los = {}
         rinvs = {}
         sss = {}
-        outs = {}
 
-        def square(w, h, cs=slice(0, WC)):
-            if (w, h) not in sqs:
-                sqs[(w, h)] = work.tile([P, WC], F32, name="sq%d" % h)
-            nc.scalar.activation(out=sqs[(w, h)][:, cs], in_=codes[(w, h)][:, cs], func=ACT.Square)
+        def square(g, h, cs=slice(0, GC)):
+            if (g, h) not in sqs:
+                sqs[(g, h)] = work.tile([P, GC], F32, name="sq%d" % h)
+            nc.scalar.activation(out=sqs[(g, h)][:, cs], in_=codes[(g, h)][:, cs], func=ACT.Square)
 
-        def add_halves(w):
-            tots[w] = work.tile([P, WC], F32, name="tot")
-            nc.gpsimd.tensor_tensor(out=tots[w][:], in0=sqs[(w, 0)][:], in1=sqs[(w, 1)][:], op=ALU.add)
+        def add_halves(g):
+            tots[g] = work.tile([P, GC], F32, name="tot")
+            nc.gpsimd.tensor_tensor(out=tots[g][:], in0=sqs[(g, 0)][:], in1=sqs[(g, 1)][:], op=ALU.add)
 
-        def high_part(w):
-            his[w] = split.tile([P, WC], BF16, name="hi")
-            nc.scalar.copy(out=his[w][:], in_=tots[w][:])
-
-        def low_part(w):
-            los[w] = split.tile([P, WC], BF16, name="lo")
-            nc.gpsimd.tensor_tensor(out=los[w][:], in0=tots[w][:], in1=his[w][:], op=ALU.subtract)
-
-        def sum_filters(w):
-            ss = aux.tile([P, WC], F32, name="ss", tag="aux")
-            nc.tensor.matmul(out=ss[:], lhsT=ones_bf[:], rhs=his[w][:], start=True, stop=False)
-            nc.tensor.matmul(out=ss[:], lhsT=ones_bf[:], rhs=los[w][:], start=False, stop=True)
-            sss[w] = ss
-
-        def rsqrt(w):
-            rinvs[w] = work.tile([P, WC], F32, name="rinv")
-            nc.scalar.activation(out=rinvs[w][:], in_=sss[w][:], func=ACT.Abs_reciprocal_sqrt)
-
-        def scale_store(w, h):
-            g, a = win[w]
-            nb = SIZES[g]
-            if a == 0:
-                outs[(g, h)] = outp.tile([P, nb, T], F32, name="o%d" % h)
-            o = outs[(g, h)]
-            if nb == 8:
-                dst = o[:].rearrange("f n (ph pl) -> f (n ph) pl", pl=L)[:, :, 4 * a : 4 * a + 4]
-                rin = rinvs[w][:].rearrange("f (m b) -> f m b", b=4)
-                cod = codes[(w, h)][:].rearrange("f (m b) -> f m b", b=4)
+        def high_part(g, own=False):
+            if own:
+                his[g] = split.tile([P, GC], BF16, name="hi_own")
             else:
-                dst = o[:].rearrange("f n p -> f (n p)")
-                rin = rinvs[w][:]
-                cod = codes[(w, h)][:]
-            nc.vector.scalar_tensor_tensor(out=dst, in0=rin, scalar=1.0e12, in1=cod, op0=ALU.min, op1=ALU.mult)
-            if a == nb // 4 - 1:
-                n0 = first_batch[g]
-                nc.sync.dma_start(
-                    out=out[n0 : n0 + nb, h * P : (h + 1) * P, :].rearrange("n f p -> f n p"),
-                    in_=o[:, :, 0 : T - 1],
-                )
+                his[g] = turn.tile([P, GC], BF16, name="hi", tag="turn")
+            nc.gpsimd.tensor_scalar(
+                out=his[g][:], in0=tots[g][:], scalar1=1.0, scalar2=0.0, op0=ALU.mult, op1=ALU.add
+            )
+
+        def low_part(g):
+            los[g] = split.tile([P, GC], BF16, name="lo")
+            nc.gpsimd.tensor_tensor(out=los[g][:], in0=tots[g][:], in1=his[g][:], op=ALU.subtract)
+
+        def sum_filters(g):
+            ss = aux.tile([P, GC], F32, name="ss", tag="aux")
+            nc.tensor.matmul(out=ss[:], lhsT=ones_bf[:], rhs=his[g][:], start=True, stop=False)
+            nc.tensor.matmul(out=ss[:], lhsT=ones_bf[:], rhs=los[g][:], start=False, stop=True)
+            sss[g] = ss
+
+        def rsqrt(g):
+            rinvs[g] = turn.tile([P, GC], F32, name="rinv", tag="turn")
+            nc.scalar.activation(out=rinvs[g][:], in_=sss[g][:], func=ACT.Abs_reciprocal_sqrt)
+
+        def scale_store(g, h):
+            o = outp.tile([P, NB, T], F32, name="o%d" % h)
+            nc.vector.scalar_tensor_tensor(
+                out=o[:].rearrange("f n p -> f (n p)"),
+                in0=rinvs[g][:],
+                scalar=1.0e12,
+                in1=codes[(g, h)][:],
+                op0=ALU.min,
+                op1=ALU.mult,
+            )
+            nc.sync.dma_start(
+                out=out[g * NB : (g + 1) * NB, h * P : (h + 1) * P, :].rearrange("n f p -> f n p"),
+                in_=o[:, :, 0 : T - 1],
+            )
 
         transposes_x(0)
-        evac_x(0, both=True)
-        transposes_x(1)
-        evac_x(1, both=True)
+        evac_x(0)
         quant_x_main(0)
         halo_copy(0)
         ps_b = aux.tile([P, P], BF16, name="ps_b", tag="aux")
         nc.tensor.transpose(ps_b[:], bias_rows[:], ident_bf[:])
         nc.vector.tensor_copy(out=bias_sb[:], in_=ps_b[:, 0:6])
-        prep_w(0)
         quant_x_halo(0)
-        half(0, 0)
-        prep_w(1)
-        passes(1, 0, 4)
-        transposes_x(2)
-        evac_x(2)
-        passes(1, 0, 3)
-        passes(1, 0, 2)
-        relu4(1, 0)
-        merge(1, 0, 3)
-        merge(1, 0, 2)
-        square(0, 0)
-        transposes_x(3)
-        evac_x(3)
-        halo_copy(1)
-        square(1, 0)
-        quant_x_main(1)
-        half(0, 1)
-        quant_x_halo(1)
-        transposes_x(4)
-        evac_x(4)
-        square(0, 1)
-        add_halves(0)
-        high_part(0)
-        low_part(0)
-        half(1, 1)
-        transposes_x(5)
+        prep_w(0)
 
-        for w in range(2, NW):
-            i = w + 3
-            ahead = i < NW
-            whole = ahead and win[i][1] == SIZES[win[i][0]] // 4 - 1
-            passes(w, 0, 4)
+        for g in range(G):
+            ahead = g >= 1 and g + 1 < G
+            passes(g, 0, 4)
             if ahead:
-                evac_x(i)
-            passes(w, 0, 3)
-            passes(w, 0, 2)
-            relu4(w, 0)
-            if whole:
-                quant_x_main(win[i][0])
-                halo_copy(win[i][0])
-            square(w - 1, 1)
-            add_halves(w - 1)
-            merge(w, 0, 3)
-            if whole:
-                quant_x_halo(win[i][0])
-            merge(w, 0, 2)
-            sum_filters(w - 2)
-            rsqrt(w - 2)
-            passes(w, 1, 4)
-            passes(w, 1, 3)
-            passes(w, 1, 2)
-            high_part(w - 1)
-            low_part(w - 1)
-            scale_store(w - 2, 0)
-            scale_store(w - 2, 1)
-            relu4(w, 1)
-            square(w, 0)
-            merge(w, 1, 3)
-            merge(w, 1, 2, pieces=(2 if w == NW - 1 else 1))
-            if w + 4 < NW:
-                transposes_x(w + 4)
+                evac_x(g + 1)
+            passes(g, 0, 3)
+            passes(g, 0, 2)
+            if g >= 2:
+                high_part(g - 2)
+                low_part(g - 2)
+            if g >= 1:
+                merge(g - 1, 1, 3)
+                merge(g - 1, 1, 2)
+            relu4(g, 0)
+            if g >= 1:
+                fix(g - 1, 1)
+                square(g - 1, 1)
+                add_halves(g - 1)
+            if ahead:
+                halo_copy(g + 1)
+            merge(g, 0, 3)
+            merge(g, 0, 2)
+            if g == 0:
+                transposes_x(1)
+                evac_x(1)
+                prep_w(1)
+                halo_copy(1)
+            if g >= 2:
+                sum_filters(g - 2)
+                rsqrt(g - 2)
+            passes(g, 1, 4)
+            passes(g, 1, 3)
+            passes(g, 1, 2)
+            if g + 1 < G:
+                quant_x_main(g + 1)
+                quant_x_halo(g + 1)
+            if g >= 2:
+                scale_store(g - 2, 0)
+                scale_store(g - 2, 1)
+            relu4(g, 1)
+            fix(g, 0)
+            square(g, 0)
+            if g + 2 < G:
+                transposes_x(g + 2)
 
-        sum_filters(NW - 2)
-        rsqrt(NW - 2)
-        w = NW - 1
-        piece = WC // 2
+        g = G - 1
+        half = GC // 2
+        high_part(G - 2, own=True)
+        low_part(G - 2)
+        merge(g, 1, 3)
+        merge(g, 1, 2, pieces=2)
+        sum_filters(G - 2)
+        rsqrt(G - 2)
         last_ss = []
         for c in range(2):
-            ss = aux.tile([P, piece], F32, name="ss_last", tag="aux")
+            ss = aux.tile([P, half], F32, name="ss_last", tag="aux")
             nc.tensor.matmul(
-                out=ss[:], lhsT=ones_f32[:], rhs=sqs[(w, 0)][:, c * piece : (c + 1) * piece], start=True, stop=False
+                out=ss[:], lhsT=ones_f32[:], rhs=sqs[(g, 0)][:, c * half : (c + 1) * half], start=True, stop=False
             )
             last_ss.append(ss)
         for c in range(2):
-            square(w, 1, slice(c * piece, (c + 1) * piece))
-        scale_store(NW - 2, 0)
-        scale_store(NW - 2, 1)
-        rinv = work.tile([P, WC], F32, name="rinv")
+            fix(g, 1, slice(c * NB // 2, (c + 1) * NB // 2))
+            square(g, 1, slice(c * half, (c + 1) * half))
+        scale_store(G - 2, 0)
+        scale_store(G - 2, 1)
+        rinv = work.tile([P, GC], F32, name="rinv_last")
         for c in range(2):
-            cs = slice(c * piece, (c + 1) * piece)
-            nc.tensor.matmul(out=last_ss[c][:], lhsT=ones_f32[:], rhs=sqs[(w, 1)][:, cs], start=False, stop=True)
+            cs = slice(c * half, (c + 1) * half)
+            nc.tensor.matmul(out=last_ss[c][:], lhsT=ones_f32[:], rhs=sqs[(g, 1)][:, cs], start=False, stop=True)
             nc.scalar.activation(out=rinv[:, cs], in_=last_ss[c][:], func=ACT.Abs_reciprocal_sqrt)
         for c in range(2):
-            cs = slice(c * piece, (c + 1) * piece)
+            cs = slice(c * half, (c + 1) * half)
             for h in range(2):
-                o = outp.tile([P, 2, T], F32, name="o_last%d" % h)
+                o = outp.tile([P, NB // 2, T], F32, name="o_last%d" % h)
                 nc.vector.scalar_tensor_tensor(
                     out=o[:].rearrange("f n p -> f (n p)"),
                     in0=rinv[:, cs],
                     scalar=1.0e12,
-                    in1=codes[(w, h)][:, cs],
+                    in1=codes[(g, h)][:, cs],
                     op0=ALU.min,
                     op1=ALU.mult,
                 )
-                n0 = B - 4 + 2 * c
+                n0 = g * NB + c * (NB // 2)
                 queue = nc.sync if h == 0 else nc.scalar
                 queue.dma_start(
-                    out=out[n0 : n0 + 2, h * P : (h + 1) * P, :].rearrange("n f p -> f n p"),
+                    out=out[n0 : n0 + NB // 2, h * P : (h + 1) * P, :].rearrange("n f p -> f n p"),
                     in_=o[:, :, 0 : T - 1],
                 )

@@ -39,18 +39,16 @@ def tile_textheading_pa_t_kernel(tc, words_emb, W2, b2, W3, b3, W4, b4, out):
         xg = ctx.enter_context(tc.tile_pool(name="xg", bufs=2))
         code_pool = ctx.enter_context(tc.tile_pool(name="code", bufs=4))
         work = ctx.enter_context(tc.tile_pool(name="work", bufs=2))
-        split = ctx.enter_context(tc.tile_pool(name="split", bufs=2))
-        turn = ctx.enter_context(tc.tile_pool(name="turn", bufs=1))
+        split = ctx.enter_context(tc.tile_pool(name="split", bufs=3))
         outp = ctx.enter_context(tc.tile_pool(name="outp", bufs=3))
         mxp = ctx.enter_context(tc.psum_pool(name="mxp", bufs=2))
         aux = ctx.enter_context(tc.psum_pool(name="aux", bufs=2))
         ctx.enter_context(tc.manual_schedule())
 
-        bias_rows = const.tile([P, P], BF16, name="bias_rows")
-        nc.vector.memset(bias_rows[:], 0.0)
+        bias_bf = {}
         for K in WIDTHS:
-            c = BIAS_COL[K]
-            nc.scalar.dma_start(out=bias_rows[c : c + 2, :], in_=b_dram[K].rearrange("(h f) -> h f", h=2))
+            bias_bf[K] = const.tile([P, 2], BF16, name="bias_bf%d" % K)
+            nc.scalar.dma_start(out=bias_bf[K][:], in_=b_dram[K].rearrange("(m h) -> m h", h=2))
         x_raw = {}
         w_raw = {}
 
@@ -62,7 +60,7 @@ def tile_textheading_pa_t_kernel(tc, words_emb, W2, b2, W3, b3, W4, b4, out):
         def load_w(h):
             for K in WIDTHS:
                 t = raw.tile([P, K * D], BF16, name="w_raw%d_%d" % (K, h))
-                nc.sync.dma_start(out=t[:], in_=w_dram[K][h * P : (h + 1) * P].rearrange("f k d -> f (k d)"))
+                nc.sync.dma_start(out=t[:], in_=w_dram[K].rearrange("(m h) k d -> h m (k d)", h=2)[h])
                 w_raw[(K, h)] = t
 
         load_x(0)
@@ -82,8 +80,6 @@ def tile_textheading_pa_t_kernel(tc, words_emb, W2, b2, W3, b3, W4, b4, out):
         nc.vector.tensor_copy(
             out=perm[:].rearrange("i (pl ph) -> i pl ph", pl=L), in_=ident[:].rearrange("i (ph pl) -> i pl ph", pl=L)
         )
-        ident_bf = const.tile([P, P], BF16, name="ident_bf")
-        nc.vector.tensor_copy(out=ident_bf[:], in_=ident[:])
         ones_bf = const.tile([P, P], BF16, name="ones_bf")
         nc.vector.memset(ones_bf[:], 1.0)
         ones_f32 = const.tile([P, P], F32, name="ones_f32")
@@ -97,6 +93,8 @@ def tile_textheading_pa_t_kernel(tc, words_emb, W2, b2, W3, b3, W4, b4, out):
         w_codes = const.tile([P, 18 * P], U32, name="w_codes", align_bytes=64)
         w_scales = const.tile([P, 18 * P], U8, name="w_scales", align_bytes=64)
         bias_sb = const.tile([P, 6], F32, name="bias_sb")
+        for K in WIDTHS:
+            nc.vector.tensor_copy(out=bias_sb[:, BIAS_COL[K] : BIAS_COL[K] + 2], in_=bias_bf[K][:])
 
         bank_tags = ["c4", "c3", "c2"]
         bank_no = [0]
@@ -164,7 +162,7 @@ def tile_textheading_pa_t_kernel(tc, words_emb, W2, b2, W3, b3, W4, b4, out):
 
         def halo_copy(g):
             rows = 3 * NB
-            nc.scalar.copy(
+            nc.vector.tensor_copy(
                 out=halos[g % 2][:].bitcast(F32).rearrange("q (r w) -> q r w", w=2 * PH)[:, 0:rows, 0 : 2 * PH - 2],
                 in_=x_grp[g][:].bitcast(F32).rearrange("q (r w) -> q r w", w=2 * PH)[:, 0:rows, 2 : 2 * PH],
             )
@@ -203,17 +201,16 @@ def tile_textheading_pa_t_kernel(tc, words_emb, W2, b2, W3, b3, W4, b4, out):
                 func=ACT.Relu,
                 bias=bias_sb[:, BIAS_COL[4] + h : BIAS_COL[4] + h + 1],
             )
-            tail = code[:].rearrange("f (n p) -> f n p", p=T)[:, :, T - 3 : T]
-            nc.scalar.activation(out=tail, in_=tail, func=ACT.Relu, scale=-1.0)
 
         def merge(g, h, K, pieces=1):
             code = codes[(g, h)]
+            nc.vector.memset(code[:].rearrange("f (n p) -> f n p", p=T)[:, :, T - K : T], 0.0)
             code_v = code[:].rearrange("f (m pl) -> f m pl", pl=L)
             acc_v = accs[(g, h, K)][:].rearrange("f (pl m) -> f m pl", pl=L)
             step = BLK // pieces
             for c in range(pieces):
                 ms = slice(c * step, (c + 1) * step)
-                for a in (4, 0) if K == 3 else (0, 4):
+                for a in range(0, L, 4):
                     nc.vector.scalar_tensor_tensor(
                         out=code_v[:, ms, a : a + 4],
                         in0=acc_v[:, ms, a : a + 4],
@@ -222,14 +219,6 @@ def tile_textheading_pa_t_kernel(tc, words_emb, W2, b2, W3, b3, W4, b4, out):
                         op0=ALU.add,
                         op1=ALU.max,
                     )
-
-        def fix(g, h, ns=slice(0, NB)):
-            nc.scalar.activation(
-                out=codes[(g, h)][:].rearrange("f (n p) -> f n p", p=T)[:, ns, T - 2],
-                in_=accs[(g, h, 2)][:].rearrange("f (pl n ph) -> f pl n ph", pl=L, n=NB)[:, L - 2, ns, PH - 1],
-                func=ACT.Relu,
-                bias=bias_sb[:, BIAS_COL[2] + h : BIAS_COL[2] + h + 1],
-            )
 
         sqs = {}
         tots = {}
@@ -247,14 +236,9 @@ def tile_textheading_pa_t_kernel(tc, words_emb, W2, b2, W3, b3, W4, b4, out):
             tots[g] = work.tile([P, GC], F32, name="tot")
             nc.gpsimd.tensor_tensor(out=tots[g][:], in0=sqs[(g, 0)][:], in1=sqs[(g, 1)][:], op=ALU.add)
 
-        def high_part(g, own=False):
-            if own:
-                his[g] = split.tile([P, GC], BF16, name="hi_own")
-            else:
-                his[g] = turn.tile([P, GC], BF16, name="hi", tag="turn")
-            nc.gpsimd.tensor_scalar(
-                out=his[g][:], in0=tots[g][:], scalar1=1.0, scalar2=0.0, op0=ALU.mult, op1=ALU.add
-            )
+        def high_part(g):
+            his[g] = split.tile([P, GC], BF16, name="hi")
+            nc.scalar.copy(out=his[g][:], in_=tots[g][:])
 
         def low_part(g):
             los[g] = split.tile([P, GC], BF16, name="lo")
@@ -267,31 +251,33 @@ def tile_textheading_pa_t_kernel(tc, words_emb, W2, b2, W3, b3, W4, b4, out):
             sss[g] = ss
 
         def rsqrt(g):
-            rinvs[g] = turn.tile([P, GC], F32, name="rinv", tag="turn")
+            rinvs[g] = work.tile([P, GC], F32, name="rinv")
             nc.scalar.activation(out=rinvs[g][:], in_=sss[g][:], func=ACT.Abs_reciprocal_sqrt)
 
+        outs = {}
+
         def scale_store(g, h):
-            o = outp.tile([P, NB, T], F32, name="o%d" % h)
+            if h == 0:
+                outs[g] = outp.tile([P, NB, 2, T - 1], F32, name="o")
+            o = outs[g]
             nc.vector.scalar_tensor_tensor(
-                out=o[:].rearrange("f n p -> f (n p)"),
-                in0=rinvs[g][:],
+                out=o[:, :, h, :],
+                in0=rinvs[g][:].rearrange("f (n p) -> f n p", p=T)[:, :, 0 : T - 1],
                 scalar=1.0e12,
-                in1=codes[(g, h)][:],
+                in1=codes[(g, h)][:].rearrange("f (n p) -> f n p", p=T)[:, :, 0 : T - 1],
                 op0=ALU.min,
                 op1=ALU.mult,
             )
-            nc.sync.dma_start(
-                out=out[g * NB : (g + 1) * NB, h * P : (h + 1) * P, :].rearrange("n f p -> f n p"),
-                in_=o[:, :, 0 : T - 1],
-            )
+            if h == 1:
+                nc.sync.dma_start(
+                    out=out[g * NB : (g + 1) * NB].rearrange("n (m h) p -> m n (h p)", h=2),
+                    in_=o[:].rearrange("m n h p -> m n (h p)"),
+                )
 
         transposes_x(0)
         evac_x(0)
         quant_x_main(0)
         halo_copy(0)
-        ps_b = aux.tile([P, P], BF16, name="ps_b", tag="aux")
-        nc.tensor.transpose(ps_b[:], bias_rows[:], ident_bf[:])
-        nc.vector.tensor_copy(out=bias_sb[:], in_=ps_b[:, 0:6])
         quant_x_halo(0)
         prep_w(0)
 
@@ -302,25 +288,22 @@ def tile_textheading_pa_t_kernel(tc, words_emb, W2, b2, W3, b3, W4, b4, out):
                 evac_x(g + 1)
             passes(g, 0, 3)
             passes(g, 0, 2)
-            if g >= 2:
-                high_part(g - 2)
-                low_part(g - 2)
-            if g >= 1:
-                merge(g - 1, 1, 3)
-                merge(g - 1, 1, 2)
             relu4(g, 0)
+            if ahead:
+                quant_x_main(g + 1)
+                halo_copy(g + 1)
             if g >= 1:
-                fix(g - 1, 1)
                 square(g - 1, 1)
                 add_halves(g - 1)
-            if ahead:
-                halo_copy(g + 1)
             merge(g, 0, 3)
+            if ahead:
+                quant_x_halo(g + 1)
             merge(g, 0, 2)
             if g == 0:
                 transposes_x(1)
                 evac_x(1)
                 prep_w(1)
+                quant_x_main(1)
                 halo_copy(1)
             if g >= 2:
                 sum_filters(g - 2)
@@ -328,26 +311,25 @@ def tile_textheading_pa_t_kernel(tc, words_emb, W2, b2, W3, b3, W4, b4, out):
             passes(g, 1, 4)
             passes(g, 1, 3)
             passes(g, 1, 2)
-            if g + 1 < G:
-                quant_x_main(g + 1)
-                quant_x_halo(g + 1)
+            if g >= 1:
+                high_part(g - 1)
+                low_part(g - 1)
             if g >= 2:
                 scale_store(g - 2, 0)
                 scale_store(g - 2, 1)
             relu4(g, 1)
-            fix(g, 0)
             square(g, 0)
+            merge(g, 1, 3)
+            if g == 0:
+                quant_x_halo(1)
+            merge(g, 1, 2, pieces=(2 if g == G - 1 else 1))
             if g + 2 < G:
                 transposes_x(g + 2)
 
-        g = G - 1
-        half = GC // 2
-        high_part(G - 2, own=True)
-        low_part(G - 2)
-        merge(g, 1, 3)
-        merge(g, 1, 2, pieces=2)
         sum_filters(G - 2)
         rsqrt(G - 2)
+        g = G - 1
+        half = GC // 2
         last_ss = []
         for c in range(2):
             ss = aux.tile([P, half], F32, name="ss_last", tag="aux")
@@ -356,30 +338,29 @@ def tile_textheading_pa_t_kernel(tc, words_emb, W2, b2, W3, b3, W4, b4, out):
             )
             last_ss.append(ss)
         for c in range(2):
-            fix(g, 1, slice(c * NB // 2, (c + 1) * NB // 2))
             square(g, 1, slice(c * half, (c + 1) * half))
         scale_store(G - 2, 0)
         scale_store(G - 2, 1)
-        rinv = work.tile([P, GC], F32, name="rinv_last")
+        rinv = work.tile([P, GC], F32, name="rinv")
         for c in range(2):
             cs = slice(c * half, (c + 1) * half)
             nc.tensor.matmul(out=last_ss[c][:], lhsT=ones_f32[:], rhs=sqs[(g, 1)][:, cs], start=False, stop=True)
             nc.scalar.activation(out=rinv[:, cs], in_=last_ss[c][:], func=ACT.Abs_reciprocal_sqrt)
         for c in range(2):
             cs = slice(c * half, (c + 1) * half)
+            o = outp.tile([P, NB // 2, 2, T - 1], F32, name="o_last")
             for h in range(2):
-                o = outp.tile([P, NB // 2, T], F32, name="o_last%d" % h)
                 nc.vector.scalar_tensor_tensor(
-                    out=o[:].rearrange("f n p -> f (n p)"),
-                    in0=rinv[:, cs],
+                    out=o[:, :, h, :],
+                    in0=rinv[:, cs].rearrange("f (n p) -> f n p", p=T)[:, :, 0 : T - 1],
                     scalar=1.0e12,
-                    in1=codes[(g, h)][:, cs],
+                    in1=codes[(g, h)][:, cs].rearrange("f (n p) -> f n p", p=T)[:, :, 0 : T - 1],
                     op0=ALU.min,
                     op1=ALU.mult,
                 )
-                n0 = g * NB + c * (NB // 2)
-                queue = nc.sync if h == 0 else nc.scalar
-                queue.dma_start(
-                    out=out[n0 : n0 + NB // 2, h * P : (h + 1) * P, :].rearrange("n f p -> f n p"),
-                    in_=o[:, :, 0 : T - 1],
-                )
+            n0 = g * NB + c * (NB // 2)
+            queue = nc.sync if c == 0 else nc.scalar
+            queue.dma_start(
+                out=out[n0 : n0 + NB // 2].rearrange("n (m h) p -> m n (h p)", h=2),
+                in_=o[:].rearrange("m n h p -> m n (h p)"),
+            )

@@ -43,7 +43,6 @@ def tile_textheading_pa_t_kernel(tc, words_emb, W2, b2, W3, b3, W4, b4, out):
         outp = ctx.enter_context(tc.tile_pool(name="outp", bufs=3))
         mxp = ctx.enter_context(tc.psum_pool(name="mxp", bufs=2))
         aux = ctx.enter_context(tc.psum_pool(name="aux", bufs=2))
-        ctx.enter_context(tc.manual_schedule())
 
         bias_bf = {}
         for K in WIDTHS:

@@ -43,11 +43,15 @@ def tile_textheading_pa_t_kernel(tc, words_emb, W2, b2, W3, b3, W4, b4, out):
         outp = ctx.enter_context(tc.tile_pool(name="outp", bufs=3))
         mxp = ctx.enter_context(tc.psum_pool(name="mxp", bufs=2))
         aux = ctx.enter_context(tc.psum_pool(name="aux", bufs=2))
+        ctx.enter_context(tc.manual_schedule())
 
-        bias_bf = {}
+        bias_words = const.tile([P, P], F32, name="bias_words")
+        nc.vector.memset(bias_words[:], 0.0)
         for K in WIDTHS:
-            bias_bf[K] = const.tile([P, 2], BF16, name="bias_bf%d" % K)
-            nc.scalar.dma_start(out=bias_bf[K][:], in_=b_dram[K].rearrange("(m h) -> m h", h=2))
+            row = BIAS_COL[K] // 2
+            nc.scalar.dma_start(
+                out=bias_words[row : row + 1, :], in_=b_dram[K].bitcast(F32).rearrange("(o m) -> o m", o=1)
+            )
         x_raw = {}
         w_raw = {}
 
@@ -92,14 +96,13 @@ def tile_textheading_pa_t_kernel(tc, words_emb, W2, b2, W3, b3, W4, b4, out):
         w_codes = const.tile([P, 18 * P], U32, name="w_codes", align_bytes=64)
         w_scales = const.tile([P, 18 * P], U8, name="w_scales", align_bytes=64)
         bias_sb = const.tile([P, 6], F32, name="bias_sb")
-        for K in WIDTHS:
-            nc.vector.tensor_copy(out=bias_sb[:, BIAS_COL[K] : BIAS_COL[K] + 2], in_=bias_bf[K][:])
+        bias_pairs = const.tile([P, 3], F32, name="bias_pairs")
 
         bank_tags = ["c4", "c3", "c2"]
         bank_no = [0]
 
-        def prep_w(h):
-            for K in WIDTHS:
+        def prep_w(h, widths=WIDTHS):
+            for K in widths:
                 words = w_raw[(K, h)][:].bitcast(F32)
                 grp = raw.tile([P, K * D], BF16, name="w_grp%d_%d" % (K, h), align_bytes=64)
                 grp_w = grp[:].bitcast(F32).rearrange("q (c f u) -> q c f u", c=K, f=P, u=2)
@@ -141,15 +144,17 @@ def tile_textheading_pa_t_kernel(tc, words_emb, W2, b2, W3, b3, W4, b4, out):
                 banks.append(ps)
             ps_x[g] = banks
 
-        def evac_x(g):
+        def evac_x(g, both=False):
             grp = xg.tile([P, L * BLK * 4], BF16, name="x_grp", align_bytes=64)
             grp_v = grp[:].bitcast(F32).rearrange("q (pl n ph u) -> q pl n ph u", pl=L, n=NB, ph=PH, u=2)
             for n in range(NB):
                 i = n % 2
-                nc.scalar.copy(
-                    out=grp_v[:, :, n, :, :],
-                    in_=ps_x[g][n // 2][:, 2 * i : 2 * i + 2, :].rearrange("q u (pl ph) -> q pl ph u", pl=L),
-                )
+                dst = grp_v[:, :, n, :, :]
+                src = ps_x[g][n // 2][:, 2 * i : 2 * i + 2, :].rearrange("q u (pl ph) -> q pl ph u", pl=L)
+                if both and n >= 2:
+                    nc.vector.tensor_copy(out=dst, in_=src)
+                else:
+                    nc.scalar.copy(out=dst, in_=src)
             x_grp[g] = grp
             x_codes[g] = xq.tile([P, NCOL], U32, name="x_codes", align_bytes=64)
             x_scales[g] = xq.tile([P, NCOL], U8, name="x_scales", align_bytes=64)
@@ -161,7 +166,7 @@ def tile_textheading_pa_t_kernel(tc, words_emb, W2, b2, W3, b3, W4, b4, out):
 
         def halo_copy(g):
             rows = 3 * NB
-            nc.vector.tensor_copy(
+            nc.scalar.copy(
                 out=halos[g % 2][:].bitcast(F32).rearrange("q (r w) -> q r w", w=2 * PH)[:, 0:rows, 0 : 2 * PH - 2],
                 in_=x_grp[g][:].bitcast(F32).rearrange("q (r w) -> q r w", w=2 * PH)[:, 0:rows, 2 : 2 * PH],
             )
@@ -237,7 +242,9 @@ def tile_textheading_pa_t_kernel(tc, words_emb, W2, b2, W3, b3, W4, b4, out):
 
         def high_part(g):
             his[g] = split.tile([P, GC], BF16, name="hi")
-            nc.scalar.copy(out=his[g][:], in_=tots[g][:])
+            nc.gpsimd.tensor_scalar(
+                out=his[g][:], in0=tots[g][:], scalar1=1.0, scalar2=0.0, op0=ALU.mult, op1=ALU.add
+            )
 
         def low_part(g):
             los[g] = split.tile([P, GC], BF16, name="lo")
@@ -274,11 +281,16 @@ def tile_textheading_pa_t_kernel(tc, words_emb, W2, b2, W3, b3, W4, b4, out):
                 )
 
         transposes_x(0)
-        evac_x(0)
+        evac_x(0, both=True)
         quant_x_main(0)
         halo_copy(0)
+        prep_w(0, (4,))
         quant_x_halo(0)
-        prep_w(0)
+        prep_w(0, (3, 2))
+        ps_b = aux.tile([P, P], F32, name="ps_b", tag="aux")
+        nc.tensor.transpose(ps_b[:], bias_words[:], ident[:])
+        nc.vector.tensor_copy(out=bias_pairs[:], in_=ps_b[:, 0:3])
+        nc.vector.tensor_copy(out=bias_sb[:], in_=bias_pairs[:].bitcast(BF16))
 
         for g in range(G):
             ahead = g >= 1 and g + 1 < G
@@ -294,6 +306,8 @@ def tile_textheading_pa_t_kernel(tc, words_emb, W2, b2, W3, b3, W4, b4, out):
             if g >= 1:
                 square(g - 1, 1)
                 add_halves(g - 1)
+                high_part(g - 1)
+                low_part(g - 1)
             merge(g, 0, 3)
             if ahead:
                 quant_x_halo(g + 1)
@@ -310,9 +324,6 @@ def tile_textheading_pa_t_kernel(tc, words_emb, W2, b2, W3, b3, W4, b4, out):
             passes(g, 1, 4)
             passes(g, 1, 3)
             passes(g, 1, 2)
-            if g >= 1:
-                high_part(g - 1)
-                low_part(g - 1)
             if g >= 2:
                 scale_store(g - 2, 0)
                 scale_store(g - 2, 1)

from contextlib import ExitStack

import concourse.mybir as mybir
from concourse.masks import make_identity

F32 = mybir.dt.float32
BF16 = mybir.dt.bfloat16
U32 = mybir.dt.uint32
U8 = mybir.dt.uint8
FP8X4 = mybir.dt.float8_e4m3fn_x4
ACT = mybir.ActivationFunctionType
ALU = mybir.AluOpType

P = 128
B, T, D, F = 32, 128, 512, 256
WIDTHS = (4, 3, 2)
NB = 4
G = B // NB
L = 8
PH = T // L
BLK = NB * PH
HALO = 4
NCOL = (L + HALO) * BLK
GC = NB * T
UNIT0 = {4: 0, 3: 4, 2: 7}
BIAS_COL = {4: 0, 3: 2, 2: 4}
QUANT_RUNS = {4: ((0, 4),), 3: ((0, 2), (2, 1)), 2: ((0, 2),)}
FLOPS = 2 * B * D * F * (2 * 127 + 3 * 126 + 4 * 125)


def tile_textheading_pa_t_kernel(tc, words_emb, W2, b2, W3, b3, W4, b4, out):
    nc = tc.nc
    w_dram = {2: W2, 3: W3, 4: W4}
    b_dram = {2: b2, 3: b3, 4: b4}
    with ExitStack() as ctx:
        const = ctx.enter_context(tc.tile_pool(name="const", bufs=1))
        raw = ctx.enter_context(tc.tile_pool(name="raw", bufs=1))
        xq = ctx.enter_context(tc.tile_pool(name="xq", bufs=3))
        xg = ctx.enter_context(tc.tile_pool(name="xg", bufs=2))
        code_pool = ctx.enter_context(tc.tile_pool(name="code", bufs=4))
        work = ctx.enter_context(tc.tile_pool(name="work", bufs=2))
        split = ctx.enter_context(tc.tile_pool(name="split", bufs=3))
        outp = ctx.enter_context(tc.tile_pool(name="outp", bufs=3))
        mxp = ctx.enter_context(tc.psum_pool(name="mxp", bufs=2))
        aux = ctx.enter_context(tc.psum_pool(name="aux", bufs=2))
        ctx.enter_context(tc.manual_schedule())

        bias_words = const.tile([P, P], F32, name="bias_words")
        nc.vector.memset(bias_words[:], 0.0)
        for K in WIDTHS:
            row = BIAS_COL[K] // 2
            nc.scalar.dma_start(
                out=bias_words[row : row + 1, :], in_=b_dram[K].bitcast(F32).rearrange("(o m) -> o m", o=1)
            )
        x_raw = {}
        w_raw = {}

        def load_x(g):
            t = raw.tile([P, NB, D], BF16, name="x_raw%d" % g)
            nc.sync.dma_start(out=t[:], in_=words_emb[g * NB : (g + 1) * NB].rearrange("n p d -> p n d"))
            x_raw[g] = t

        def load_w(h):
            for K in WIDTHS:
                t = raw.tile([P, K * D], BF16, name="w_raw%d_%d" % (K, h))
                nc.sync.dma_start(out=t[:], in_=w_dram[K].rearrange("(m h) k d -> h m (k d)", h=2)[h])
                w_raw[(K, h)] = t

        load_x(0)
        load_w(0)
        load_x(1)
        load_w(1)
        for g in range(2, G):
            load_x(g)

        one_col = const.tile([P, 1], F32, name="one_col")
        nc.vector.memset(one_col[:], 1.0)
        dummy = const.tile([P, 1], F32, name="dummy")
        nc.scalar.activation(out=dummy[:], in_=one_col[:], func=ACT.Abs_reciprocal_sqrt)
        ident = const.tile([P, P], F32, name="ident")
        make_identity(nc, ident[:])
        perm = const.tile([P, P], F32, name="perm")
        nc.vector.tensor_copy(
            out=perm[:].rearrange("i (pl ph) -> i pl ph", pl=L), in_=ident[:].rearrange("i (ph pl) -> i pl ph", pl=L)
        )
        ones_bf = const.tile([P, P], BF16, name="ones_bf")
        nc.vector.memset(ones_bf[:], 1.0)
        ones_f32 = const.tile([P, P], F32, name="ones_f32")
        nc.vector.memset(ones_f32[:], 1.0)
        halos = []
        for i in range(2):
            halo = const.tile([P, HALO * BLK * 4], BF16, name="halo%d" % i, align_bytes=64)
            nc.vector.memset(halo[:], 0.0)
            halos.append(halo)

        w_codes = const.tile([P, 18 * P], U32, name="w_codes", align_bytes=64)
        w_scales = const.tile([P, 18 * P], U8, name="w_scales", align_bytes=64)
        bias_sb = const.tile([P, 6], F32, name="bias_sb")
        bias_pairs = const.tile([P, 3], F32, name="bias_pairs")

        bank_tags = ["c4", "c3", "c2"]
        bank_no = [0]

        def prep_w(h, widths=WIDTHS):
            for K in widths:
                words = w_raw[(K, h)][:].bitcast(F32)
                grp = raw.tile([P, K * D], BF16, name="w_grp%d_%d" % (K, h), align_bytes=64)
                grp_w = grp[:].bitcast(F32).rearrange("q (c f u) -> q c f u", c=K, f=P, u=2)
                for k0 in range(0, K, 2):
                    cnt = min(2, K - k0)
                    ps = mxp.tile([P, 4, P], F32, name="ps_w", tag=bank_tags[bank_no[0] % 3])
                    for i in range(cnt):
                        for u in range(2):
                            col = (k0 + i) * 256 + u * P
                            nc.tensor.transpose(ps[:, 2 * i + u, :], words[:, col : col + P], ident[:])
                    src = ps[:, 0 : 2 * cnt, :].rearrange("q (c u) f -> q c f u", u=2)
                    if k0 == 0:
                        nc.scalar.copy(out=grp_w[:, k0 : k0 + cnt], in_=src)
                    else:
                        nc.vector.tensor_copy(out=grp_w[:, k0 : k0 + cnt], in_=src)
                    bank_no[0] += 1
                unit = h * 9 + UNIT0[K]
                for k0, cnt in QUANT_RUNS[K]:
                    cols = slice((unit + k0) * P, (unit + k0 + cnt) * P)
                    nc.vector.quantize_mx(
                        out=w_codes[:, cols].bitcast(FP8X4),
                        scales=w_scales[:, cols],
                        in_=grp[:, k0 * D : (k0 + cnt) * D],
                    )

        ps_x = {}
        x_grp = {}
        x_codes = {}
        x_scales = {}

        def transposes_x(g):
            words = x_raw[g][:].bitcast(F32)
            banks = []
            for n0 in range(0, NB, 2):
                ps = aux.tile([P, 4, P], F32, name="ps_x", tag="aux")
                for i in range(2):
                    for u in range(2):
                        nc.tensor.transpose(ps[:, 2 * i + u, :], words[:, n0 + i, u * P : (u + 1) * P], perm[:])
                banks.append(ps)
            ps_x[g] = banks

        def evac_x(g, both=False):
            grp = xg.tile([P, L * BLK * 4], BF16, name="x_grp", align_bytes=64)
            grp_v = grp[:].bitcast(F32).rearrange("q (pl n ph u) -> q pl n ph u", pl=L, n=NB, ph=PH, u=2)
            for n in range(NB):
                i = n % 2
                dst = grp_v[:, :, n, :, :]
                src = ps_x[g][n // 2][:, 2 * i : 2 * i + 2, :].rearrange("q u (pl ph) -> q pl ph u", pl=L)
                if both and n >= 2:
                    nc.vector.tensor_copy(out=dst, in_=src)
                else:
                    nc.scalar.copy(out=dst, in_=src)
            x_grp[g] = grp
            x_codes[g] = xq.tile([P, NCOL], U32, name="x_codes", align_bytes=64)
            x_scales[g] = xq.tile([P, NCOL], U8, name="x_scales", align_bytes=64)

        def quant_x_main(g):
            nc.vector.quantize_mx(
                out=x_codes[g][:, 0 : L * BLK].bitcast(FP8X4), scales=x_scales[g][:, 0 : L * BLK], in_=x_grp[g][:]
            )

        def halo_copy(g):
            rows = 3 * NB
            nc.scalar.copy(
                out=halos[g % 2][:].bitcast(F32).rearrange("q (r w) -> q r w", w=2 * PH)[:, 0:rows, 0 : 2 * PH - 2],
                in_=x_grp[g][:].bitcast(F32).rearrange("q (r w) -> q r w", w=2 * PH)[:, 0:rows, 2 : 2 * PH],
            )

        def quant_x_halo(g):
            nc.vector.quantize_mx(
                out=x_codes[g][:, L * BLK : NCOL].bitcast(FP8X4),
                scales=x_scales[g][:, L * BLK : NCOL],
                in_=halos[g % 2][:],
            )

        accs = {}
        codes = {}

        def passes(g, h, K):
            acc = mxp.tile([P, 512], F32, name="acc", tag="c%d" % K)
            for k in range(K):
                unit = h * 9 + UNIT0[K] + k
                nc.tensor.matmul_mx(
                    out=acc[:],
                    lhsT=w_codes[:, unit * P : (unit + 1) * P].bitcast(FP8X4),
                    lhsT_scale=w_scales[:, unit * P : (unit + 1) * P],
                    rhs=x_codes[g][:, k * BLK : k * BLK + 512].bitcast(FP8X4),
                    rhs_scale=x_scales[g][:, k * BLK : k * BLK + 512],
                    start=(k == 0),
                    stop=(k == K - 1),
                )
            accs[(g, h, K)] = acc

        def relu4(g, h):
            code = code_pool.tile([P, GC], F32, name="code%d" % h)
            codes[(g, h)] = code
            nc.scalar.activation(
                out=code[:].rearrange("f (m a b) -> f a m b", a=L // 4, b=4),
                in_=accs[(g, h, 4)][:].rearrange("f (a b m) -> f a m b", a=L // 4, b=4),
                func=ACT.Relu,
                bias=bias_sb[:, BIAS_COL[4] + h : BIAS_COL[4] + h + 1],
            )

        def merge(g, h, K, pieces=1):
            code = codes[(g, h)]
            nc.vector.memset(code[:].rearrange("f (n p) -> f n p", p=T)[:, :, T - K : T], 0.0)
            code_v = code[:].rearrange("f (m pl) -> f m pl", pl=L)
            acc_v = accs[(g, h, K)][:].rearrange("f (pl m) -> f m pl", pl=L)
            step = BLK // pieces
            for c in range(pieces):
                ms = slice(c * step, (c + 1) * step)
                for a in range(0, L, 4):
                    nc.vector.scalar_tensor_tensor(
                        out=code_v[:, ms, a : a + 4],
                        in0=acc_v[:, ms, a : a + 4],
                        scalar=bias_sb[:, BIAS_COL[K] + h : BIAS_COL[K] + h + 1],
                        in1=code_v[:, ms, a : a + 4],
                        op0=ALU.add,
                        op1=ALU.max,
                    )

        sqs = {}
        tots = {}
        his = {}
        los = {}
        rinvs = {}
        sss = {}

        def square(g, h, cs=slice(0, GC)):
            if (g, h) not in sqs:
                sqs[(g, h)] = work.tile([P, GC], F32, name="sq%d" % h)
            nc.scalar.activation(out=sqs[(g, h)][:, cs], in_=codes[(g, h)][:, cs], func=ACT.Square)

        def add_halves(g):
            tots[g] = work.tile([P, GC], F32, name="tot")
            nc.gpsimd.tensor_tensor(out=tots[g][:], in0=sqs[(g, 0)][:], in1=sqs[(g, 1)][:], op=ALU.add)

        def high_part(g):
            his[g] = split.tile([P, GC], BF16, name="hi")
            nc.gpsimd.tensor_scalar(
                out=his[g][:], in0=tots[g][:], scalar1=1.0, scalar2=0.0, op0=ALU.mult, op1=ALU.add
            )

        def low_part(g):
            los[g] = split.tile([P, GC], BF16, name="lo")
            nc.gpsimd.tensor_tensor(out=los[g][:], in0=tots[g][:], in1=his[g][:], op=ALU.subtract)

        def sum_filters(g):
            ss = aux.tile([P, GC], F32, name="ss", tag="aux")
            nc.tensor.matmul(out=ss[:], lhsT=ones_bf[:], rhs=his[g][:], start=True, stop=False)
            nc.tensor.matmul(out=ss[:], lhsT=ones_bf[:], rhs=los[g][:], start=False, stop=True)
            sss[g] = ss

        def rsqrt(g):
            rinvs[g] = work.tile([P, GC], F32, name="rinv")
            nc.scalar.activation(out=rinvs[g][:], in_=sss[g][:], func=ACT.Abs_reciprocal_sqrt)

        outs = {}

        def scale_store(g, h):
            if h == 0:
                outs[g] = outp.tile([P, NB, 2, T - 1], F32, name="o")
            o = outs[g]
            nc.vector.scalar_tensor_tensor(
                out=o[:, :, h, :],
                in0=rinvs[g][:].rearrange("f (n p) -> f n p", p=T)[:, :, 0 : T - 1],
                scalar=1.0e12,
                in1=codes[(g, h)][:].rearrange("f (n p) -> f n p", p=T)[:, :, 0 : T - 1],
                op0=ALU.min,
                op1=ALU.mult,
            )
            if h == 1:
                nc.sync.dma_start(
                    out=out[g * NB : (g + 1) * NB].rearrange("n (m h) p -> m n (h p)", h=2),
                    in_=o[:].rearrange("m n h p -> m n (h p)"),
                )

        transposes_x(0)
        evac_x(0, both=True)
        quant_x_main(0)
        halo_copy(0)
        prep_w(0, (4,))
        quant_x_halo(0)
        prep_w(0, (3, 2))
        ps_b = aux.tile([P, P], F32, name="ps_b", tag="aux")
        nc.tensor.transpose(ps_b[:], bias_words[:], ident[:])
        nc.vector.tensor_copy(out=bias_pairs[:], in_=ps_b[:, 0:3])
        nc.vector.tensor_copy(out=bias_sb[:], in_=bias_pairs[:].bitcast(BF16))

        for g in range(G):
            ahead = g >= 1 and g + 1 < G
            passes(g, 0, 4)
            if ahead:
                evac_x(g + 1)
            passes(g, 0, 3)
            passes(g, 0, 2)
            relu4(g, 0)
            if ahead:
                quant_x_main(g + 1)
                halo_copy(g + 1)
            if g >= 1:
                square(g - 1, 1)
                add_halves(g - 1)
                high_part(g - 1)
                low_part(g - 1)
            merge(g, 0, 3)
            if ahead:
                quant_x_halo(g + 1)
            merge(g, 0, 2)
            if g == 0:
                transposes_x(1)
                evac_x(1)
                prep_w(1)
                quant_x_main(1)
                halo_copy(1)
            if g >= 2:
                sum_filters(g - 2)
                rsqrt(g - 2)
            passes(g, 1, 4)
            passes(g, 1, 3)
            passes(g, 1, 2)
            if g >= 2:
                scale_store(g - 2, 0)
                scale_store(g - 2, 1)
            relu4(g, 1)
            square(g, 0)
            merge(g, 1, 3)
            if g == 0:
                quant_x_halo(1)
            merge(g, 1, 2, pieces=(2 if g == G - 1 else 1))
            if g + 2 < G:
                transposes_x(g + 2)

        sum_filters(G - 2)
        rsqrt(G - 2)
        g = G - 1
        half = GC // 2
        last_ss = []
        for c in range(2):
            ss = aux.tile([P, half], F32, name="ss_last", tag="aux")
            nc.tensor.matmul(
                out=ss[:], lhsT=ones_f32[:], rhs=sqs[(g, 0)][:, c * half : (c + 1) * half], start=True, stop=False
            )
            last_ss.append(ss)
        for c in range(2):
            square(g, 1, slice(c * half, (c + 1) * half))
        scale_store(G - 2, 0)
        scale_store(G - 2, 1)
        rinv = work.tile([P, GC], F32, name="rinv")
        for c in range(2):
            cs = slice(c * half, (c + 1) * half)
            nc.tensor.matmul(out=last_ss[c][:], lhsT=ones_f32[:], rhs=sqs[(g, 1)][:, cs], start=False, stop=True)
            nc.scalar.activation(out=rinv[:, cs], in_=last_ss[c][:], func=ACT.Abs_reciprocal_sqrt)
        for c in range(2):
            cs = slice(c * half, (c + 1) * half)
            o = outp.tile([P, NB // 2, 2, T - 1], F32, name="o_last")
            for h in range(2):
                nc.vector.scalar_tensor_tensor(
                    out=o[:, :, h, :],
                    in0=rinv[:, cs].rearrange("f (n p) -> f n p", p=T)[:, :, 0 : T - 1],
                    scalar=1.0e12,
                    in1=codes[(g, h)][:, cs].rearrange("f (n p) -> f n p", p=T)[:, :, 0 : T - 1],
                    op0=ALU.min,
                    op1=ALU.mult,
                )
            n0 = g * NB + c * (NB // 2)
            queue = nc.sync if c == 0 else nc.scalar
            queue.dma_start(
                out=out[n0 : n0 + NB // 2].rearrange("n (m h) p -> m n (h p)", h=2),
                in_=o[:].rearrange("m n h p -> m n (h p)"),
            )
